import numpy as np
import ml_dtypes


def mxq(x, axis, fmt="e4m3"):
    dtype, down = {"e4m3": (ml_dtypes.float8_e4m3fn, 7), "e5m2": (ml_dtypes.float8_e5m2, 14)}[fmt]
    v = np.moveaxis(np.asarray(x, np.float32).astype(ml_dtypes.bfloat16).astype(np.float64), axis, -1)
    blocks = v.reshape(v.shape[:-1] + (-1, 32))
    amax = np.abs(blocks).max(-1, keepdims=True)
    byte = np.maximum(np.where(amax > 0, np.frexp(amax)[1] - 1 + 127, 0) - down, 1)
    scale = np.exp2(byte - 127.0)
    codes = (blocks / scale).astype(np.float32).astype(dtype).astype(np.float64)
    return np.moveaxis((codes * scale).reshape(v.shape), -1, axis)


WIDE = False


def mx_kscale(k):
    if not WIDE:
        return np.ones(k)
    levels = np.array([10, -10, 5, -5, 0])
    if k % 512:
        return np.exp2(np.random.permutation(np.resize(levels, k // 32))).repeat(32)
    a = np.empty((k // 512, 16))
    for p in range(k // 512):
        a[p, :8] = np.random.permutation(np.resize(levels, 8))
        for g in range(8):
            far = levels[np.abs(levels - a[p, g]) >= 10]
            a[p, g + 8] = far[np.random.randint(len(far))]
    return np.exp2(a.ravel()).repeat(32)


BF16 = ml_dtypes.bfloat16


def bf(x):
    return np.asarray(x, np.float32).astype(BF16)


def f64(x):
    return np.asarray(x).astype(np.float64)


N, S, K, Yd, Xd = 1024, 4, 16, 1024, 512
LOG_2PI = np.log(2.0 * np.pi)


def softplus(v):
    return np.maximum(v, 0.0) + np.log(1.0 + np.exp(-np.abs(v)))


def log_softmax(v, axis):
    m = v - v.max(axis, keepdims=True)
    return m - np.log(np.exp(m).sum(axis, keepdims=True))


def mv_gaussian_log_prob(value, mu, sig_diags, event_shape):
    diff = value - mu
    M = np.sum((diff / sig_diags) ** 2, axis=-1)
    half_log_det = np.sum(np.log(sig_diags), axis=-1)
    return -0.5 * (event_shape * LOG_2PI + M) - half_log_det


def setup_inputs():
    s = mx_kscale(Yd)
    return {"Y": bf(np.random.standard_normal((N, Yd)) * 0.5 * s),
            "We_mu": bf(np.random.standard_normal((Yd, Xd)) * 2.0 / np.sqrt(Yd) / s[:, None]),
            "be_mu": bf(np.random.standard_normal(Xd) * 0.1),
            "We_sig": bf(np.random.standard_normal((Yd, Xd)) * 1.0 / np.sqrt(Yd) / s[:, None]),
            "be_sig": bf(-3.0 + np.random.standard_normal(Xd) * 0.1),
            "phi_mus": bf(np.random.standard_normal((K, Xd)) * 3.0 / np.sqrt(Xd)),
            "phi_sigs": bf(1.0 + (np.random.random_sample((K, Xd)) - 0.5) * 9.0 / np.sqrt(Xd)),
            "phi_logits": bf(np.random.standard_normal(K))}


def reference(Y, We_mu, be_mu, We_sig, be_sig, phi_mus, phi_sigs, phi_logits):
    Yq = mxq(f64(Y), 1, "e4m3")
    enc_mu = (Yq @ mxq(f64(We_mu), 0, "e4m3")) + f64(be_mu)
    enc_sig = softplus((Yq @ mxq(f64(We_sig), 0, "e4m3")) + f64(be_sig)) + 1e-3
    log_pi = log_softmax(f64(phi_logits), -1)
    std_k = enc_sig[:, None, :] + f64(phi_sigs)[None, :, :]
    z_logits = log_pi[None, :] + mv_gaussian_log_prob(enc_mu[:, None, :], f64(phi_mus)[None, :, :], std_k, Xd)
    z_log_probs = log_softmax(z_logits, -1)
    return enc_mu, enc_sig, z_log_probs

@@ -1,0 +1,421 @@
+from contextlib import ExitStack
+
+import concourse.mybir as mybir
+from concourse.masks import make_identity
+
+F32 = mybir.dt.float32
+BF16 = mybir.dt.bfloat16
+U32 = mybir.dt.uint32
+U8 = mybir.dt.uint8
+FP8X4 = mybir.dt.float8_e4m3fn_x4
+ACT = mybir.ActivationFunctionType
+ALU = mybir.AluOpType
+AX = mybir.AxisListType
+
+P = 128
+ROWS = 1024
+KDIM = 1024
+D = 512
+CLUSTERS = 16
+ROW_TILES = ROWS // P
+D_CHUNKS = D // P
+PACK = 4
+PASSES = KDIM // (P * PACK)
+HALF = 512
+HALVES = ROWS // HALF
+PSUM_BANKS = 8
+TILES_PER_BANK = HALF // P
+BANKS_PER_CLUSTER = ROW_TILES // TILES_PER_BANK
+PAIRS_PER_HALF = HALF // (2 * P)
+
+BATCH = 4
+LOGS_AHEAD = PSUM_BANKS // BANKS_PER_CLUSTER - 2
+SCALAR_SQUARES = 2
+GPSIMD_SQUARES = 1
+FIRST_SQUARED = CLUSTERS - SCALAR_SQUARES - GPSIMD_SQUARES
+LOG_TILES = BATCH + 1
+
+EPS = 0.001
+CAP = 40.0
+
+ROW_MU = 0
+ROW_SIG = CLUSTERS
+ROW_BE_MU = 2 * CLUSTERS
+ROW_BE_SIG = 2 * CLUSTERS + 1
+
+FLOPS = 2 * 2 * ROWS * KDIM * D
+
+
+def part(i, size):
+    return slice(i * size, (i + 1) * size)
+
+
+def tile_deepgmm_pa_kernel(
+    tc, Y, We_mu, be_mu, We_sig, be_sig, phi_mus, phi_sigs, phi_logits, out_0, out_1, out_2
+):
+    nc = tc.nc
+    with ExitStack() as ctx:
+        ctx.enter_context(tc.manual_schedule())
+        keep = ctx.enter_context(tc.tile_pool(name="keep", bufs=1))
+        stage = ctx.enter_context(tc.tile_pool(name="stage", bufs=ROW_TILES))
+        psum = ctx.enter_context(tc.psum_pool(name="psum", bufs=PSUM_BANKS))
+
+        ident_f32 = keep.tile([P, P], F32)
+        make_identity(nc, ident_f32[:])
+        ident_bf16 = keep.tile([P, P], BF16)
+        make_identity(nc, ident_bf16[:])
+        ones_col = keep.tile([P, 1], F32)
+        nc.vector.memset(ones_col[:], 1.0)
+
+        param_rows = keep.tile([P, D], BF16)
+        nc.vector.memset(param_rows[:], 0.0)
+        nc.scalar.dma_start(out=param_rows[ROW_MU : ROW_MU + CLUSTERS, :], in_=phi_mus)
+        nc.scalar.dma_start(out=param_rows[ROW_SIG : ROW_SIG + CLUSTERS, :], in_=phi_sigs)
+        nc.scalar.dma_start(out=param_rows[ROW_BE_MU : ROW_BE_MU + 1, :], in_=be_mu.unsqueeze(0))
+        nc.scalar.dma_start(out=param_rows[ROW_BE_SIG : ROW_BE_SIG + 1, :], in_=be_sig.unsqueeze(0))
+        logits_bc = keep.tile([P, CLUSTERS], BF16)
+        nc.scalar.dma_start(out=logits_bc[:], in_=phi_logits.partition_broadcast(P))
+
+        cols = keep.tile([P, D_CHUNKS, P], F32)
+        sig_t = keep.tile([P, D_CHUNKS, ROWS], F32)
+        mu_t = keep.tile([P, D_CHUNKS, ROWS], F32)
+        be_sig_less_cap = keep.tile([P, D_CHUNKS], F32)
+        neg_half_cols = keep.tile([P, D_CHUNKS, CLUSTERS], F32)
+        sums = keep.tile([P, CLUSTERS, ROW_TILES], F32)
+
+        with ExitStack() as head:
+            load = head.enter_context(tc.tile_pool(name="load", bufs=1))
+            soft = head.enter_context(tc.tile_pool(name="soft", bufs=1))
+            codes_pool = head.enter_context(tc.tile_pool(name="codes", bufs=1))
+            y_codes = codes_pool.tile([P, PASSES, ROWS], U32, align_bytes=64)
+            y_scales = codes_pool.tile([P, PASSES, ROWS], U8, align_bytes=64)
+            sig_codes = codes_pool.tile([P, PASSES, D], U32, align_bytes=64)
+            sig_scales = codes_pool.tile([P, PASSES, D], U8, align_bytes=64)
+            mu_codes = codes_pool.tile([P, PASSES, D], U32, align_bytes=64)
+            mu_scales = codes_pool.tile([P, PASSES, D], U8, align_bytes=64)
+
+            y_raw = load.tile([P, ROW_TILES, KDIM], BF16)
+            y_grouped = load.tile([P, PASSES, ROWS, PACK], BF16, align_bytes=64)
+            sig_raw = load.tile([P, PASSES, PACK, D], BF16)
+            sig_grouped = load.tile([P, PASSES, D, PACK], BF16, align_bytes=64)
+            mu_raw = load.tile([P, PASSES, PACK, D], BF16)
+            mu_grouped = load.tile([P, PASSES, D, PACK], BF16, align_bytes=64)
+            nc.sync.dma_start(
+                out=sig_raw[:], in_=We_sig.rearrange("(g p t) d -> p g t d", g=PASSES, p=P, t=PACK)
+            )
+            y_view = Y.rearrange("(j p) y -> p j y", p=P)
+            for pair in range(ROW_TILES // 2):
+                nc.sync.dma_start(out=y_raw[:, part(pair, 2), :], in_=y_view[:, part(pair, 2), :])
+            nc.sync.dma_start(
+                out=mu_raw[:], in_=We_mu.rearrange("(g p t) d -> p g t d", g=PASSES, p=P, t=PACK)
+            )
+
+            params_t = psum.tile([P, D_CHUNKS, P], BF16, tag="bank")
+            for c in range(D_CHUNKS):
+                nc.tensor.transpose(
+                    out=params_t[:, c, :], in_=param_rows[:, part(c, P)], identity=ident_bf16[:]
+                )
+            nc.vector.tensor_copy(out=cols[:], in_=params_t[:])
+            nc.vector.tensor_scalar(
+                out=be_sig_less_cap[:],
+                in0=cols[:, :, ROW_BE_SIG],
+                scalar1=CAP,
+                scalar2=None,
+                op0=ALU.subtract,
+            )
+            nc.vector.tensor_scalar(
+                out=neg_half_cols[:],
+                in0=cols[:, :, ROW_MU : ROW_MU + CLUSTERS],
+                scalar1=-0.5,
+                scalar2=None,
+                op0=ALU.mult,
+            )
+
+            def quantise_weight(grouped, codes, scales):
+                for g in range(PASSES):
+                    nc.vector.quantize_mx(
+                        out=codes[:, g, :].bitcast(FP8X4),
+                        scales=scales[:, g, :],
+                        in_=grouped[:, g].rearrange("p d t -> p (d t)"),
+                    )
+
+            for g in range(PASSES):
+                nc.vector.tensor_copy(
+                    out=sig_grouped[:, g],
+                    in_=sig_raw[:, g].rearrange("p t d -> p d t"),
+                )
+            quantise_weight(sig_grouped, sig_codes, sig_scales)
+            for g in range(PASSES):
+                nc.gpsimd.tensor_scalar(
+                    out=mu_grouped[:, g],
+                    in0=mu_raw[:, g].rearrange("p t d -> p d t"),
+                    scalar1=1.0,
+                    scalar2=0.0,
+                    op0=ALU.mult,
+                    op1=ALU.add,
+                )
+
+            y_words = y_raw[:].bitcast(F32)
+            y_pairs = y_grouped[:].bitcast(F32)
+            for h in range(HALVES):
+                for pair in range(PAIRS_PER_HALF * h, PAIRS_PER_HALF * (h + 1)):
+                    for g in range(PASSES):
+                        y_t = psum.tile([P, 2, 2 * P], F32, tag="bank")
+                        for u in range(2):
+                            for jj in range(2):
+                                nc.tensor.transpose(
+                                    out=y_t[:, u, part(jj, P)],
+                                    in_=y_words[:, 2 * pair + jj, 2 * P * g + u : 2 * P * (g + 1) : 2],
+                                    identity=ident_f32[:],
+                                )
+                        nc.scalar.copy(
+                            out=y_pairs[:, g, part(pair, 2 * P), :],
+                            in_=y_t[:].rearrange("p u n -> p n u"),
+                        )
+                for g in range(PASSES):
+                    nc.vector.quantize_mx(
+                        out=y_codes[:, g, part(h, HALF)].bitcast(FP8X4),
+                        scales=y_scales[:, g, part(h, HALF)],
+                        in_=y_grouped[:, g, part(h, HALF), :].rearrange("p n t -> p (n t)"),
+                    )
+
+            def project(codes, scales, c, h):
+                acc = psum.tile([P, HALF], F32, tag="bank")
+                for g in range(PASSES):
+                    nc.tensor.matmul_mx(
+                        out=acc[:],
+                        lhsT=codes[:, g, part(c, P)].bitcast(FP8X4),
+                        lhsT_scale=scales[:, g, part(c, P)],
+                        rhs=y_codes[:, g, part(h, HALF)].bitcast(FP8X4),
+                        rhs_scale=y_scales[:, g, part(h, HALF)],
+                        start=(g == 0),
+                        stop=(g == PASSES - 1),
+                    )
+                return acc
+
+            curve = soft.tile([P, D_CHUNKS, ROWS], F32)
+            excess = soft.tile([P, D_CHUNKS, ROWS], F32)
+            sig_accs = {}
+            for h in range(HALVES):
+                for c in range(D_CHUNKS):
+                    sig_accs[c, h] = project(sig_codes, sig_scales, c, h)
+                    nc.vector.tensor_scalar(
+                        out=curve[:, c, part(h, HALF)],
+                        in0=sig_accs[c, h][:],
+                        scalar1=cols[:, c, ROW_BE_SIG : ROW_BE_SIG + 1],
+                        scalar2=CAP,
+                        op0=ALU.add,
+                        op1=ALU.min,
+                    )
+                    nc.scalar.activation(
+                        out=curve[:, c, part(h, HALF)], in_=curve[:, c, part(h, HALF)], func=ACT.Exp
+                    )
+            for h in range(HALVES):
+                for c in range(D_CHUNKS):
+                    nc.vector.tensor_scalar(
+                        out=excess[:, c, part(h, HALF)],
+                        in0=sig_accs[c, h][:],
+                        scalar1=be_sig_less_cap[:, c : c + 1],
+                        scalar2=0.0,
+                        op0=ALU.add,
+                        op1=ALU.max,
+                    )
+            for c in range(D_CHUNKS):
+                nc.scalar.activation(out=curve[:, c, :], in_=curve[:, c, :], func=ACT.Ln, bias=ones_col[:])
+                nc.vector.scalar_tensor_tensor(
+                    out=sig_t[:, c, :],
+                    in0=curve[:, c, :],
+                    scalar=EPS,
+                    in1=excess[:, c, :],
+                    op0=ALU.add,
+                    op1=ALU.add,
+                )
+            quantise_weight(mu_grouped, mu_codes, mu_scales)
+            for c in range(D_CHUNKS):
+                for h in range(HALVES):
+                    acc = project(mu_codes, mu_scales, c, h)
+                    nc.vector.tensor_scalar(
+                        out=mu_t[:, c, part(h, HALF)],
+                        in0=acc[:],
+                        scalar1=cols[:, c, ROW_BE_MU : ROW_BE_MU + 1],
+                        scalar2=None,
+                        op0=ALU.add,
+                    )
+
+        def store_rows(src, dst):
+            for j in range(ROW_TILES):
+                rows_t = psum.tile([P, D], F32, tag="bank")
+                for c in range(D_CHUNKS):
+                    nc.tensor.transpose(
+                        out=rows_t[:, part(c, P)], in_=src[:, c, part(j, P)], identity=ident_f32[:]
+                    )
+                rows_sb = stage.tile([P, D], F32)
+                nc.vector.tensor_copy(out=rows_sb[:], in_=rows_t[:])
+                nc.sync.dma_start(out=dst[part(j, P), :], in_=rows_sb[:])
+
+        log_ring = ctx.enter_context(tc.tile_pool(name="log_ring", bufs=LOG_TILES, reuse_waits="tile"))
+        term_ring = ctx.enter_context(tc.tile_pool(name="term_ring", bufs=BATCH, reuse_waits="tile"))
+        square_pool = ctx.enter_context(tc.tile_pool(name="square_pool", bufs=GPSIMD_SQUARES, reuse_waits="tile"))
+        log_tiles = {}
+        term_tiles = {}
+        square_tiles = {}
+        banks = {}
+
+        def scalar_squares(k):
+            return CLUSTERS - SCALAR_SQUARES <= k < CLUSTERS
+
+        def logs(k):
+            log_std = log_ring.tile([P, D_CHUNKS, ROWS], F32)
+            log_tiles[k] = log_std
+            for c in range(D_CHUNKS):
+                nc.scalar.activation(
+                    out=log_std[:, c, :],
+                    in_=sig_t[:, c, :],
+                    func=ACT.Ln,
+                    bias=cols[:, c, ROW_SIG + k : ROW_SIG + k + 1],
+                )
+
+        def inverse_powers(k):
+            term = term_ring.tile([P, D_CHUNKS, ROWS], F32)
+            term_tiles[k] = term
+            power = -2.0 if k >= FIRST_SQUARED else -1.0
+            for c in range(D_CHUNKS):
+                nc.scalar.activation(
+                    out=term[:, c, :], in_=log_tiles[k][:, c, :], func=ACT.Exp, scale=power
+                )
+
+        def quarter_squares_on_scalar(k):
+            quarter = log_ring.tile([P, D_CHUNKS, ROWS], F32, tag="log_std")
+            square_tiles[k] = quarter
+            for c in range(D_CHUNKS):
+                nc.scalar.activation(
+                    out=quarter[:, c, :],
+                    in_=mu_t[:, c, :],
+                    func=ACT.Square,
+                    scale=0.5,
+                    bias=neg_half_cols[:, c, k : k + 1],
+                )
+
+        def quarter_squares_on_gpsimd(k):
+            quarter = square_pool.tile([P, D_CHUNKS, ROWS], F32)
+            square_tiles[k] = quarter
+            for c in range(D_CHUNKS):
+                nc.gpsimd.tensor_scalar(
+                    out=quarter[:, c, :],
+                    in0=mu_t[:, c, :],
+                    scalar1=0.5,
+                    scalar2=neg_half_cols[:, c, k : k + 1],
+                    op0=ALU.mult,
+                    op1=ALU.add,
+                )
+            for c in range(D_CHUNKS):
+                nc.gpsimd.tensor_tensor(
+                    out=quarter[:, c, :], in0=quarter[:, c, :], in1=quarter[:, c, :], op=ALU.mult
+                )
+
+        def weigh_squares(k):
+            term = term_tiles[k]
+            for c in range(D_CHUNKS):
+                nc.vector.scalar_tensor_tensor(
+                    out=term[:, c, :],
+                    in0=square_tiles[k][:, c, :],
+                    scalar=2.0,
+                    in1=term[:, c, :],
+                    op0=ALU.mult,
+                    op1=ALU.mult,
+                )
+
+        def weigh(k):
+            term = term_tiles[k]
+            for c in range(D_CHUNKS):
+                nc.vector.scalar_tensor_tensor(
+                    out=term[:, c, :],
+                    in0=mu_t[:, c, :],
+                    scalar=cols[:, c, ROW_MU + k : ROW_MU + k + 1],
+                    in1=term[:, c, :],
+                    op0=ALU.subtract,
+                    op1=ALU.mult,
+                )
+            for c in range(D_CHUNKS):
+                nc.vector.scalar_tensor_tensor(
+                    out=term[:, c, :],
+                    in0=term[:, c, :],
+                    scalar=0.5,
+                    in1=term[:, c, :],
+                    op0=ALU.mult,
+                    op1=ALU.mult,
+                )
+
+        def fold(src, k, opens, closes):
+            for c in range(D_CHUNKS):
+                for j in range(ROW_TILES):
+                    nc.tensor.matmul(
+                        out=banks[k][j // TILES_PER_BANK][:, j % TILES_PER_BANK, :],
+                        lhsT=src[:, c, part(j, P)],
+                        rhs=ident_f32[:],
+                        is_transpose=True,
+                        start=(opens and c == 0 and j % TILES_PER_BANK == 0),
+                        stop=(closes and c == D_CHUNKS - 1 and j % TILES_PER_BANK == TILES_PER_BANK - 1),
+                    )
+
+        def fold_logs(k):
+            bank_a = psum.tile([P, TILES_PER_BANK, P], F32, tag="bank")
+            bank_b = psum.tile([P, TILES_PER_BANK, P], F32, tag="bank")
+            banks[k] = [bank_a, bank_b]
+            fold(log_tiles[k], k, True, False)
+
+        def finish_sums(k):
+            for b in range(BANKS_PER_CLUSTER):
+                nc.vector.tensor_reduce(
+                    out=sums[:, k, part(b, TILES_PER_BANK)], in_=banks[k][b][:], axis=AX.X, op=ALU.add
+                )
+
+        for k in range(BATCH):
+            logs(k)
+        for k in range(FIRST_SQUARED, FIRST_SQUARED + GPSIMD_SQUARES):
+            quarter_squares_on_gpsimd(k)
+        store_rows(mu_t, out_0)
+        store_rows(sig_t, out_1)
+        for k in range(LOGS_AHEAD):
+            fold_logs(k)
+        for first in range(0, CLUSTERS, BATCH):
+            for k in range(first, first + BATCH):
+                inverse_powers(k)
+            for k in range(first, first + BATCH):
+                if k + LOGS_AHEAD < CLUSTERS:
+                    fold_logs(k + LOGS_AHEAD)
+                if k >= FIRST_SQUARED:
+                    weigh_squares(k)
+                else:
+                    weigh(k)
+                fold(term_tiles[k], k, False, True)
+                if k + BATCH < CLUSTERS:
+                    logs(k + BATCH)
+                elif scalar_squares(k + 1):
+                    quarter_squares_on_scalar(k + 1)
+                if k >= 1:
+                    finish_sums(k - 1)
+        finish_sums(CLUSTERS - 1)
+
+        shape = [P, ROW_TILES, CLUSTERS]
+        z = keep.tile(shape, F32)
+        nc.vector.tensor_tensor(
+            out=z[:],
+            in0=logits_bc[:].unsqueeze(1).to_broadcast(shape),
+            in1=sums[:].rearrange("p k j -> p j k"),
+            op=ALU.subtract,
+        )
+        top = keep.tile([P, ROW_TILES], F32)
+        nc.vector.tensor_reduce(out=top[:], in_=z[:], axis=AX.X, op=ALU.max)
+        nc.vector.tensor_tensor(
+            out=z[:], in0=z[:], in1=top[:].unsqueeze(2).to_broadcast(shape), op=ALU.subtract
+        )
+        weights = keep.tile(shape, F32)
+        nc.scalar.activation(out=weights[:], in_=z[:], func=ACT.Exp)
+        norm = keep.tile([P, ROW_TILES], F32)
+        nc.vector.tensor_reduce(out=norm[:], in_=weights[:], axis=AX.X, op=ALU.add)
+        nc.scalar.activation(out=norm[:], in_=norm[:], func=ACT.Ln)
+        nc.vector.tensor_tensor(
+            out=z[:], in0=z[:], in1=norm[:].unsqueeze(2).to_broadcast(shape), op=ALU.subtract
+        )
+        nc.sync.dma_start(out=out_2.rearrange("(j p) k -> p j k", p=P), in_=z[:])

@@ -23,20 +23,15 @@ PACK = 4
 PASSES = KDIM // (P * PACK)
 HALF = 512
 HALVES = ROWS // HALF
-PSUM_BANKS = 8
-TILES_PER_BANK = HALF // P
-BANKS_PER_CLUSTER = ROW_TILES // TILES_PER_BANK
+TILES_PER_HALF = HALF // P
 PAIRS_PER_HALF = HALF // (2 * P)
+UNITS = HALVES * CLUSTERS
 
-BATCH = 4
-LOGS_AHEAD = PSUM_BANKS // BANKS_PER_CLUSTER - 2
-SCALAR_SQUARES = 2
-GPSIMD_SQUARES = 1
-FIRST_SQUARED = CLUSTERS - SCALAR_SQUARES - GPSIMD_SQUARES
-LOG_TILES = BATCH + 1
+RING = 12
+SCALAR_LAG = 5
 
 EPS = 0.001
-CAP = 40.0
+TINY = 2.0**-60
 
 ROW_MU = 0
 ROW_SIG = CLUSTERS
@@ -50,6 +45,10 @@ def part(i, size):
     return slice(i * size, (i + 1) * size)
 
 
+def squared_by_scalar(t):
+    return t % 2 == 1 and t < 30
+
+
 def tile_deepgmm_pa_kernel(
     tc, Y, We_mu, be_mu, We_sig, be_sig, phi_mus, phi_sigs, phi_logits, out_0, out_1, out_2
 ):
@@ -57,15 +56,19 @@ def tile_deepgmm_pa_kernel(
     with ExitStack() as ctx:
         ctx.enter_context(tc.manual_schedule())
         keep = ctx.enter_context(tc.tile_pool(name="keep", bufs=1))
-        stage = ctx.enter_context(tc.tile_pool(name="stage", bufs=ROW_TILES))
-        psum = ctx.enter_context(tc.psum_pool(name="psum", bufs=PSUM_BANKS))
+        stage = ctx.enter_context(tc.tile_pool(name="stage", bufs=8))
+        psum_a = ctx.enter_context(tc.psum_pool(name="psum_a", bufs=4))
+        psum_b = ctx.enter_context(tc.psum_pool(name="psum_b", bufs=2))
+        psum_c = ctx.enter_context(tc.psum_pool(name="psum_c", bufs=2))
 
         ident_f32 = keep.tile([P, P], F32)
         make_identity(nc, ident_f32[:])
         ident_bf16 = keep.tile([P, P], BF16)
         make_identity(nc, ident_bf16[:])
-        ones_col = keep.tile([P, 1], F32)
-        nc.vector.memset(ones_col[:], 1.0)
+        ones = keep.tile([P, P], F32)
+        nc.vector.memset(ones[:], 1.0)
+        warm = keep.tile([P, 1], F32)
+        nc.scalar.activation(out=warm[:], in_=ones[:, 0:1], func=ACT.Sigmoid)
 
         param_rows = keep.tile([P, D], BF16)
         nc.vector.memset(param_rows[:], 0.0)
@@ -73,78 +76,72 @@ def tile_deepgmm_pa_kernel(
         nc.scalar.dma_start(out=param_rows[ROW_SIG : ROW_SIG + CLUSTERS, :], in_=phi_sigs)
         nc.scalar.dma_start(out=param_rows[ROW_BE_MU : ROW_BE_MU + 1, :], in_=be_mu.unsqueeze(0))
         nc.scalar.dma_start(out=param_rows[ROW_BE_SIG : ROW_BE_SIG + 1, :], in_=be_sig.unsqueeze(0))
-        logits_bc = keep.tile([P, CLUSTERS], BF16)
-        nc.scalar.dma_start(out=logits_bc[:], in_=phi_logits.partition_broadcast(P))
 
         cols = keep.tile([P, D_CHUNKS, P], F32)
-        sig_t = keep.tile([P, D_CHUNKS, ROWS], F32)
-        mu_t = keep.tile([P, D_CHUNKS, ROWS], F32)
-        be_sig_less_cap = keep.tile([P, D_CHUNKS], F32)
-        neg_half_cols = keep.tile([P, D_CHUNKS, CLUSTERS], F32)
+        neg_be_sig = keep.tile([P, D_CHUNKS], F32)
+        mu_cols = keep.tile([P, D_CHUNKS, CLUSTERS], F32)
+        inv_phi = keep.tile([P, D_CHUNKS, CLUSTERS], F32)
+        inv_phi_sq = keep.tile([P, D_CHUNKS, CLUSTERS], F32)
+        log_phi = keep.tile([P, D_CHUNKS, CLUSTERS], F32)
+        logits_bc = keep.tile([P, CLUSTERS], BF16)
+        be_mu_bc = keep.tile([P, D], BF16)
+        curve = keep.tile([P, D_CHUNKS, ROWS], F32)
+        neg_sig = keep.tile([P, D_CHUNKS, ROWS], F32)
+        products = keep.tile([P, UNITS, HALF], F32)
         sums = keep.tile([P, CLUSTERS, ROW_TILES], F32)
+        y_codes = keep.tile([P, PASSES, ROWS], U32, align_bytes=64)
+        y_scales = keep.tile([P, PASSES, ROWS], U8, align_bytes=64)
+        mu_codes = keep.tile([P, PASSES, D], U32, align_bytes=64)
+        mu_scales = keep.tile([P, PASSES, D], U8, align_bytes=64)
+
+        def matmul_y_moving(acc, codes, scales, c, h):
+            for g in range(PASSES):
+                nc.tensor.matmul_mx(
+                    out=acc[:],
+                    lhsT=codes[:, g, part(c, P)].bitcast(FP8X4),
+                    lhsT_scale=scales[:, g, part(c, P)],
+                    rhs=y_codes[:, g, part(h, HALF)].bitcast(FP8X4),
+                    rhs_scale=y_scales[:, g, part(h, HALF)],
+                    start=(g == 0),
+                    stop=(g == PASSES - 1),
+                )
 
         with ExitStack() as head:
             load = head.enter_context(tc.tile_pool(name="load", bufs=1))
-            soft = head.enter_context(tc.tile_pool(name="soft", bufs=1))
-            codes_pool = head.enter_context(tc.tile_pool(name="codes", bufs=1))
-            y_codes = codes_pool.tile([P, PASSES, ROWS], U32, align_bytes=64)
-            y_scales = codes_pool.tile([P, PASSES, ROWS], U8, align_bytes=64)
-            sig_codes = codes_pool.tile([P, PASSES, D], U32, align_bytes=64)
-            sig_scales = codes_pool.tile([P, PASSES, D], U8, align_bytes=64)
-            mu_codes = codes_pool.tile([P, PASSES, D], U32, align_bytes=64)
-            mu_scales = codes_pool.tile([P, PASSES, D], U8, align_bytes=64)
-
             y_raw = load.tile([P, ROW_TILES, KDIM], BF16)
             y_grouped = load.tile([P, PASSES, ROWS, PACK], BF16, align_bytes=64)
             sig_raw = load.tile([P, PASSES, PACK, D], BF16)
             sig_grouped = load.tile([P, PASSES, D, PACK], BF16, align_bytes=64)
+            sig_codes = load.tile([P, PASSES, D], U32, align_bytes=64)
+            sig_scales = load.tile([P, PASSES, D], U8, align_bytes=64)
             mu_raw = load.tile([P, PASSES, PACK, D], BF16)
             mu_grouped = load.tile([P, PASSES, D, PACK], BF16, align_bytes=64)
-            nc.sync.dma_start(
-                out=sig_raw[:], in_=We_sig.rearrange("(g p t) d -> p g t d", g=PASSES, p=P, t=PACK)
-            )
+
             y_view = Y.rearrange("(j p) y -> p j y", p=P)
-            for pair in range(ROW_TILES // 2):
+            sig_view = We_sig.rearrange("(g p t) d -> p g t d", g=PASSES, p=P, t=PACK)
+            for g in range(PASSES):
+                nc.sync.dma_start(out=sig_raw[:, g], in_=sig_view[:, g])
+                nc.sync.dma_start(out=y_raw[:, part(g, 2), :], in_=y_view[:, part(g, 2), :])
+            for pair in range(PAIRS_PER_HALF, ROW_TILES // 2):
                 nc.sync.dma_start(out=y_raw[:, part(pair, 2), :], in_=y_view[:, part(pair, 2), :])
-            nc.sync.dma_start(
-                out=mu_raw[:], in_=We_mu.rearrange("(g p t) d -> p g t d", g=PASSES, p=P, t=PACK)
-            )
-
-            params_t = psum.tile([P, D_CHUNKS, P], BF16, tag="bank")
-            for c in range(D_CHUNKS):
-                nc.tensor.transpose(
-                    out=params_t[:, c, :], in_=param_rows[:, part(c, P)], identity=ident_bf16[:]
-                )
-            nc.vector.tensor_copy(out=cols[:], in_=params_t[:])
-            nc.vector.tensor_scalar(
-                out=be_sig_less_cap[:],
-                in0=cols[:, :, ROW_BE_SIG],
-                scalar1=CAP,
-                scalar2=None,
-                op0=ALU.subtract,
-            )
-            nc.vector.tensor_scalar(
-                out=neg_half_cols[:],
-                in0=cols[:, :, ROW_MU : ROW_MU + CLUSTERS],
-                scalar1=-0.5,
-                scalar2=None,
-                op0=ALU.mult,
-            )
-
-            def quantise_weight(grouped, codes, scales):
-                for g in range(PASSES):
-                    nc.vector.quantize_mx(
-                        out=codes[:, g, :].bitcast(FP8X4),
-                        scales=scales[:, g, :],
-                        in_=grouped[:, g].rearrange("p d t -> p (d t)"),
-                    )
+            nc.sync.dma_start(out=mu_raw[:], in_=We_mu.rearrange("(g p t) d -> p g t d", g=PASSES, p=P, t=PACK))
+            nc.sync.dma_start(out=be_mu_bc[:], in_=be_mu.partition_broadcast(P))
+            nc.sync.dma_start(out=logits_bc[:], in_=phi_logits.partition_broadcast(P))
 
             for g in range(PASSES):
-                nc.vector.tensor_copy(
+                nc.vector.tensor_scalar(
                     out=sig_grouped[:, g],
-                    in_=sig_raw[:, g].rearrange("p t d -> p d t"),
+                    in0=sig_raw[:, g].rearrange("p t d -> p d t"),
+                    scalar1=-1.0,
+                    scalar2=None,
+                    op0=ALU.mult,
                 )
-            quantise_weight(sig_grouped, sig_codes, sig_scales)
+            for g in range(PASSES):
+                nc.vector.quantize_mx(
+                    out=sig_codes[:, g, :].bitcast(FP8X4),
+                    scales=sig_scales[:, g, :],
+                    in_=sig_grouped[:, g].rearrange("p d t -> p (d t)"),
+                )
             for g in range(PASSES):
                 nc.gpsimd.tensor_scalar(
                     out=mu_grouped[:, g],
@@ -157,21 +154,23 @@ def tile_deepgmm_pa_kernel(
 
             y_words = y_raw[:].bitcast(F32)
             y_pairs = y_grouped[:].bitcast(F32)
-            for h in range(HALVES):
-                for pair in range(PAIRS_PER_HALF * h, PAIRS_PER_HALF * (h + 1)):
-                    for g in range(PASSES):
-                        y_t = psum.tile([P, 2, 2 * P], F32, tag="bank")
-                        for u in range(2):
-                            for jj in range(2):
-                                nc.tensor.transpose(
-                                    out=y_t[:, u, part(jj, P)],
-                                    in_=y_words[:, 2 * pair + jj, 2 * P * g + u : 2 * P * (g + 1) : 2],
-                                    identity=ident_f32[:],
-                                )
-                        nc.scalar.copy(
-                            out=y_pairs[:, g, part(pair, 2 * P), :],
-                            in_=y_t[:].rearrange("p u n -> p n u"),
-                        )
+
+            def turn_y(pair, pool):
+                for g in range(PASSES):
+                    y_t = pool.tile([P, 2, 2 * P], F32, tag="bank")
+                    for u in range(2):
+                        for jj in range(2):
+                            nc.tensor.transpose(
+                                out=y_t[:, u, part(jj, P)],
+                                in_=y_words[:, 2 * pair + jj, 2 * P * g + u : 2 * P * (g + 1) : 2],
+                                identity=ident_f32[:],
+                            )
+                    nc.scalar.copy(
+                        out=y_pairs[:, g, part(pair, 2 * P), :],
+                        in_=y_t[:].rearrange("p u n -> p n u"),
+                    )
+
+            def quantise_y(h):
                 for g in range(PASSES):
                     nc.vector.quantize_mx(
                         out=y_codes[:, g, part(h, HALF)].bitcast(FP8X4),
@@ -179,232 +178,241 @@ def tile_deepgmm_pa_kernel(
                         in_=y_grouped[:, g, part(h, HALF), :].rearrange("p n t -> p (n t)"),
                     )
 
-            def project(codes, scales, c, h):
-                acc = psum.tile([P, HALF], F32, tag="bank")
-                for g in range(PASSES):
-                    nc.tensor.matmul_mx(
-                        out=acc[:],
-                        lhsT=codes[:, g, part(c, P)].bitcast(FP8X4),
-                        lhsT_scale=scales[:, g, part(c, P)],
-                        rhs=y_codes[:, g, part(h, HALF)].bitcast(FP8X4),
-                        rhs_scale=y_scales[:, g, part(h, HALF)],
-                        start=(g == 0),
-                        stop=(g == PASSES - 1),
-                    )
-                return acc
+            for pair in range(PAIRS_PER_HALF):
+                turn_y(pair, psum_a)
+            quantise_y(0)
+            for pair in range(PAIRS_PER_HALF, ROW_TILES // 2):
+                turn_y(pair, psum_b)
 
-            curve = soft.tile([P, D_CHUNKS, ROWS], F32)
-            excess = soft.tile([P, D_CHUNKS, ROWS], F32)
+            params_t = psum_c.tile([P, D_CHUNKS, P], BF16, tag="bank")
+            for c in range(D_CHUNKS):
+                nc.tensor.transpose(out=params_t[:, c, :], in_=param_rows[:, part(c, P)], identity=ident_bf16[:])
+            nc.vector.tensor_copy(out=cols[:], in_=params_t[:])
+            nc.vector.tensor_scalar(
+                out=neg_be_sig[:], in0=cols[:, :, ROW_BE_SIG], scalar1=-1.0, scalar2=None, op0=ALU.mult
+            )
+
             sig_accs = {}
+            for c in range(D_CHUNKS):
+                acc = psum_a.tile([P, HALF], F32, tag="bank")
+                sig_accs[c, 0] = acc
+                matmul_y_moving(acc, sig_codes, sig_scales, c, 0)
+            quantise_y(1)
+            for c in range(D_CHUNKS):
+                pool = psum_b if c < 2 else psum_c
+                acc = pool.tile([P, HALF], F32, tag="bank")
+                sig_accs[c, 1] = acc
+                matmul_y_moving(acc, sig_codes, sig_scales, c, 1)
+
+            nc.vector.tensor_tensor(
+                out=mu_cols[:],
+                in0=cols[:, :, ROW_MU : ROW_MU + CLUSTERS],
+                in1=cols[:, :, ROW_BE_MU : ROW_BE_MU + 1].to_broadcast([P, D_CHUNKS, CLUSTERS]),
+                op=ALU.subtract,
+            )
+            nc.vector.reciprocal(out=inv_phi[:], in_=cols[:, :, ROW_SIG : ROW_SIG + CLUSTERS])
+            for g in range(PASSES):
+                nc.vector.quantize_mx(
+                    out=mu_codes[:, g, :].bitcast(FP8X4),
+                    scales=mu_scales[:, g, :],
+                    in_=mu_grouped[:, g].rearrange("p d t -> p (d t)"),
+                )
+            nc.vector.tensor_tensor(out=inv_phi_sq[:], in0=inv_phi[:], in1=inv_phi[:], op=ALU.mult)
+
             for h in range(HALVES):
                 for c in range(D_CHUNKS):
-                    sig_accs[c, h] = project(sig_codes, sig_scales, c, h)
-                    nc.vector.tensor_scalar(
+                    nc.scalar.activation(
                         out=curve[:, c, part(h, HALF)],
+                        in_=sig_accs[c, h][:],
+                        func=ACT.Sigmoid,
+                        bias=neg_be_sig[:, c : c + 1],
+                    )
+            for h in range(HALVES):
+                for c in range(D_CHUNKS):
+                    nc.scalar.activation(
+                        out=curve[:, c, part(h, HALF)], in_=curve[:, c, part(h, HALF)], func=ACT.Ln, bias=TINY
+                    )
+                    nc.vector.scalar_tensor_tensor(
+                        out=neg_sig[:, c, part(h, HALF)],
                         in0=sig_accs[c, h][:],
-                        scalar1=cols[:, c, ROW_BE_SIG : ROW_BE_SIG + 1],
-                        scalar2=CAP,
-                        op0=ALU.add,
+                        scalar=cols[:, c, ROW_BE_SIG : ROW_BE_SIG + 1],
+                        in1=curve[:, c, part(h, HALF)],
+                        op0=ALU.subtract,
                         op1=ALU.min,
                     )
-                    nc.scalar.activation(
-                        out=curve[:, c, part(h, HALF)], in_=curve[:, c, part(h, HALF)], func=ACT.Exp
-                    )
             for h in range(HALVES):
-                for c in range(D_CHUNKS):
-                    nc.vector.tensor_scalar(
-                        out=excess[:, c, part(h, HALF)],
-                        in0=sig_accs[c, h][:],
-                        scalar1=be_sig_less_cap[:, c : c + 1],
-                        scalar2=0.0,
-                        op0=ALU.add,
-                        op1=ALU.max,
-                    )
-            for c in range(D_CHUNKS):
-                nc.scalar.activation(out=curve[:, c, :], in_=curve[:, c, :], func=ACT.Ln, bias=ones_col[:])
-                nc.vector.scalar_tensor_tensor(
-                    out=sig_t[:, c, :],
-                    in0=curve[:, c, :],
-                    scalar=EPS,
-                    in1=excess[:, c, :],
-                    op0=ALU.add,
-                    op1=ALU.add,
+                nc.scalar.activation(
+                    out=curve[:, :, part(h, HALF)],
+                    in_=neg_sig[:, :, part(h, HALF)],
+                    func=ACT.Ln,
+                    scale=-1.0,
+                    bias=EPS,
                 )
-            quantise_weight(mu_grouped, mu_codes, mu_scales)
+            nc.scalar.activation(out=log_phi[:], in_=cols[:, :, ROW_SIG : ROW_SIG + CLUSTERS], func=ACT.Ln)
+
+        for j in range(ROW_TILES):
+            rows_mu = psum_a.tile([P, D], F32, tag="bank")
+            for g in range(PASSES):
+                nc.tensor.matmul_mx(
+                    out=rows_mu[:],
+                    lhsT=y_codes[:, g, part(j, P)].bitcast(FP8X4),
+                    lhsT_scale=y_scales[:, g, part(j, P)],
+                    rhs=mu_codes[:, g, :].bitcast(FP8X4),
+                    rhs_scale=mu_scales[:, g, :],
+                    start=(g == 0),
+                    stop=(g == PASSES - 1),
+                )
+            rows_sb = stage.tile([P, D], F32)
+            nc.vector.tensor_tensor(out=rows_sb[:], in0=rows_mu[:], in1=be_mu_bc[:], op=ALU.add)
+            nc.sync.dma_start(out=out_0[part(j, P), :], in_=rows_sb[:])
+
+        mu_accs = {}
+
+        def project_mu(h):
             for c in range(D_CHUNKS):
-                for h in range(HALVES):
-                    acc = project(mu_codes, mu_scales, c, h)
-                    nc.vector.tensor_scalar(
-                        out=mu_t[:, c, part(h, HALF)],
-                        in0=acc[:],
-                        scalar1=cols[:, c, ROW_BE_MU : ROW_BE_MU + 1],
-                        scalar2=None,
-                        op0=ALU.add,
-                    )
+                acc = psum_a.tile([P, HALF], F32, tag="bank")
+                mu_accs[c, h] = acc
+                matmul_y_moving(acc, mu_codes, mu_scales, c, h)
 
-        def store_rows(src, dst):
-            for j in range(ROW_TILES):
-                rows_t = psum.tile([P, D], F32, tag="bank")
-                for c in range(D_CHUNKS):
-                    nc.tensor.transpose(
-                        out=rows_t[:, part(c, P)], in_=src[:, c, part(j, P)], identity=ident_f32[:]
-                    )
-                rows_sb = stage.tile([P, D], F32)
-                nc.vector.tensor_copy(out=rows_sb[:], in_=rows_t[:])
-                nc.sync.dma_start(out=dst[part(j, P), :], in_=rows_sb[:])
+        project_mu(0)
 
-        log_ring = ctx.enter_context(tc.tile_pool(name="log_ring", bufs=LOG_TILES, reuse_waits="tile"))
-        term_ring = ctx.enter_context(tc.tile_pool(name="term_ring", bufs=BATCH, reuse_waits="tile"))
-        square_pool = ctx.enter_context(tc.tile_pool(name="square_pool", bufs=GPSIMD_SQUARES, reuse_waits="tile"))
-        log_tiles = {}
-        term_tiles = {}
-        square_tiles = {}
+        for j in range(ROW_TILES):
+            rows_t = psum_b.tile([P, D], F32, tag="bank")
+            for c in range(D_CHUNKS):
+                nc.tensor.transpose(out=rows_t[:, part(c, P)], in_=neg_sig[:, c, part(j, P)], identity=ident_f32[:])
+            rows_sb = stage.tile([P, D], F32)
+            nc.vector.tensor_scalar(
+                out=rows_sb[:], in0=rows_t[:], scalar1=-1.0, scalar2=EPS, op0=ALU.mult, op1=ALU.add
+            )
+            nc.sync.dma_start(out=out_1[part(j, P), :], in_=rows_sb[:])
+
+        phi_sums = psum_c.tile([P, CLUSTERS], F32, tag="bank")
+        for c in range(D_CHUNKS):
+            nc.tensor.matmul(
+                out=phi_sums[:], lhsT=ones[:], rhs=log_phi[:, c, :], start=(c == 0), stop=(c == D_CHUNKS - 1)
+            )
+        base = keep.tile([P, CLUSTERS], F32)
+        nc.vector.tensor_tensor(out=base[:], in0=logits_bc[:], in1=phi_sums[:], op=ALU.subtract)
+
+        ring = ctx.enter_context(tc.tile_pool(name="ring", bufs=RING, reuse_waits="tile"))
+        pair_ring = ctx.enter_context(tc.tile_pool(name="pair_ring", bufs=2, reuse_waits="tile"))
+        tiles = {}
         banks = {}
 
-        def scalar_squares(k):
-            return CLUSTERS - SCALAR_SQUARES <= k < CLUSTERS
-
-        def logs(k):
-            log_std = log_ring.tile([P, D_CHUNKS, ROWS], F32)
-            log_tiles[k] = log_std
+        def ratios(t):
+            h, k = divmod(t, CLUSTERS)
+            tile = ring.tile([P, D_CHUNKS, HALF], F32)
+            tiles[t] = tile
             for c in range(D_CHUNKS):
                 nc.scalar.activation(
-                    out=log_std[:, c, :],
-                    in_=sig_t[:, c, :],
-                    func=ACT.Ln,
-                    bias=cols[:, c, ROW_SIG + k : ROW_SIG + k + 1],
+                    out=tile[:, c, :],
+                    in_=curve[:, c, part(h, HALF)],
+                    func=ACT.Sigmoid,
+                    scale=-1.0,
+                    bias=log_phi[:, c, k : k + 1],
                 )
 
-        def inverse_powers(k):
-            term = term_ring.tile([P, D_CHUNKS, ROWS], F32)
-            term_tiles[k] = term
-            power = -2.0 if k >= FIRST_SQUARED else -1.0
-            for c in range(D_CHUNKS):
-                nc.scalar.activation(
-                    out=term[:, c, :], in_=log_tiles[k][:, c, :], func=ACT.Exp, scale=power
-                )
+        def multiply_ratios(t):
+            pairs = pair_ring.tile([P, 2, HALF], F32)
+            nc.gpsimd.tensor_tensor(out=pairs[:], in0=tiles[t][:, 0:2, :], in1=tiles[t][:, 2:4, :], op=ALU.mult)
+            nc.gpsimd.tensor_tensor(out=products[:, t, :], in0=pairs[:, 0, :], in1=pairs[:, 1, :], op=ALU.mult)
 
-        def quarter_squares_on_scalar(k):
-            quarter = log_ring.tile([P, D_CHUNKS, ROWS], F32, tag="log_std")
-            square_tiles[k] = quarter
-            for c in range(D_CHUNKS):
-                nc.scalar.activation(
-                    out=quarter[:, c, :],
-                    in_=mu_t[:, c, :],
-                    func=ACT.Square,
-                    scale=0.5,
-                    bias=neg_half_cols[:, c, k : k + 1],
-                )
-
-        def quarter_squares_on_gpsimd(k):
-            quarter = square_pool.tile([P, D_CHUNKS, ROWS], F32)
-            square_tiles[k] = quarter
-            for c in range(D_CHUNKS):
-                nc.gpsimd.tensor_scalar(
-                    out=quarter[:, c, :],
-                    in0=mu_t[:, c, :],
-                    scalar1=0.5,
-                    scalar2=neg_half_cols[:, c, k : k + 1],
-                    op0=ALU.mult,
-                    op1=ALU.add,
-                )
-            for c in range(D_CHUNKS):
-                nc.gpsimd.tensor_tensor(
-                    out=quarter[:, c, :], in0=quarter[:, c, :], in1=quarter[:, c, :], op=ALU.mult
-                )
-
-        def weigh_squares(k):
-            term = term_tiles[k]
+        def weigh(t):
+            h, k = divmod(t, CLUSTERS)
             for c in range(D_CHUNKS):
                 nc.vector.scalar_tensor_tensor(
-                    out=term[:, c, :],
-                    in0=square_tiles[k][:, c, :],
-                    scalar=2.0,
-                    in1=term[:, c, :],
-                    op0=ALU.mult,
-                    op1=ALU.mult,
-                )
-
-        def weigh(k):
-            term = term_tiles[k]
-            for c in range(D_CHUNKS):
-                nc.vector.scalar_tensor_tensor(
-                    out=term[:, c, :],
-                    in0=mu_t[:, c, :],
-                    scalar=cols[:, c, ROW_MU + k : ROW_MU + k + 1],
-                    in1=term[:, c, :],
+                    out=tiles[t][:, c, :],
+                    in0=mu_accs[c, h][:],
+                    scalar=mu_cols[:, c, k : k + 1],
+                    in1=tiles[t][:, c, :],
                     op0=ALU.subtract,
                     op1=ALU.mult,
                 )
-            for c in range(D_CHUNKS):
-                nc.vector.scalar_tensor_tensor(
-                    out=term[:, c, :],
-                    in0=term[:, c, :],
-                    scalar=0.5,
-                    in1=term[:, c, :],
-                    op0=ALU.mult,
-                    op1=ALU.mult,
-                )
 
-        def fold(src, k, opens, closes):
+        def square(t):
+            k = t % CLUSTERS
             for c in range(D_CHUNKS):
-                for j in range(ROW_TILES):
-                    nc.tensor.matmul(
-                        out=banks[k][j // TILES_PER_BANK][:, j % TILES_PER_BANK, :],
-                        lhsT=src[:, c, part(j, P)],
-                        rhs=ident_f32[:],
-                        is_transpose=True,
-                        start=(opens and c == 0 and j % TILES_PER_BANK == 0),
-                        stop=(closes and c == D_CHUNKS - 1 and j % TILES_PER_BANK == TILES_PER_BANK - 1),
+                if squared_by_scalar(t):
+                    nc.scalar.activation(
+                        out=tiles[t][:, c, :], in_=tiles[t][:, c, :], func=ACT.Square, scale=inv_phi[:, c, k : k + 1]
+                    )
+                else:
+                    nc.vector.scalar_tensor_tensor(
+                        out=tiles[t][:, c, :],
+                        in0=tiles[t][:, c, :],
+                        scalar=inv_phi_sq[:, c, k : k + 1],
+                        in1=tiles[t][:, c, :],
+                        op0=ALU.mult,
+                        op1=ALU.mult,
                     )
 
-        def fold_logs(k):
-            bank_a = psum.tile([P, TILES_PER_BANK, P], F32, tag="bank")
-            bank_b = psum.tile([P, TILES_PER_BANK, P], F32, tag="bank")
-            banks[k] = [bank_a, bank_b]
-            fold(log_tiles[k], k, True, False)
+        def fold(t):
+            bank = psum_b.tile([P, TILES_PER_HALF, P], F32, tag="bank")
+            banks[t] = bank
+            for c in range(D_CHUNKS):
+                for j in range(TILES_PER_HALF):
+                    nc.tensor.matmul(
+                        out=bank[:, j, :],
+                        lhsT=tiles[t][:, c, part(j, P)],
+                        rhs=ident_f32[:],
+                        is_transpose=True,
+                        start=(c == 0 and j == 0),
+                        stop=(c == D_CHUNKS - 1 and j == TILES_PER_HALF - 1),
+                    )
 
-        def finish_sums(k):
-            for b in range(BANKS_PER_CLUSTER):
-                nc.vector.tensor_reduce(
-                    out=sums[:, k, part(b, TILES_PER_BANK)], in_=banks[k][b][:], axis=AX.X, op=ALU.add
+        def finish(t):
+            h, k = divmod(t, CLUSTERS)
+            nc.vector.tensor_reduce(
+                out=sums[:, k, part(h, TILES_PER_HALF)], in_=banks[t][:], axis=AX.X, op=ALU.add
+            )
+
+        log_sums = keep.tile([P, CLUSTERS, ROW_TILES], F32)
+
+        def sum_logs(t):
+            h, k = divmod(t, CLUSTERS)
+            turned = psum_c.tile([P, TILES_PER_HALF, P], F32, tag="bank")
+            for j in range(TILES_PER_HALF):
+                nc.tensor.transpose(out=turned[:, j, :], in_=products[:, t, part(j, P)], identity=ident_f32[:])
+            for j in range(TILES_PER_HALF):
+                jj = h * TILES_PER_HALF + j
+                nc.scalar.activation(
+                    out=products[:, t, part(j, P)],
+                    in_=turned[:, j, :],
+                    func=ACT.Ln,
+                    accum_out=log_sums[:, k, jj : jj + 1],
                 )
 
-        for k in range(BATCH):
-            logs(k)
-        for k in range(FIRST_SQUARED, FIRST_SQUARED + GPSIMD_SQUARES):
-            quarter_squares_on_gpsimd(k)
-        store_rows(mu_t, out_0)
-        store_rows(sig_t, out_1)
-        for k in range(LOGS_AHEAD):
-            fold_logs(k)
-        for first in range(0, CLUSTERS, BATCH):
-            for k in range(first, first + BATCH):
-                inverse_powers(k)
-            for k in range(first, first + BATCH):
-                if k + LOGS_AHEAD < CLUSTERS:
-                    fold_logs(k + LOGS_AHEAD)
-                if k >= FIRST_SQUARED:
-                    weigh_squares(k)
-                else:
-                    weigh(k)
-                fold(term_tiles[k], k, False, True)
-                if k + BATCH < CLUSTERS:
-                    logs(k + BATCH)
-                elif scalar_squares(k + 1):
-                    quarter_squares_on_scalar(k + 1)
-                if k >= 1:
-                    finish_sums(k - 1)
-        finish_sums(CLUSTERS - 1)
+        for i in range(UNITS + SCALAR_LAG + 2):
+            if i < UNITS:
+                ratios(i)
+                multiply_ratios(i)
+            if 0 <= i - 1 < UNITS:
+                if i - 1 == CLUSTERS:
+                    project_mu(1)
+                weigh(i - 1)
+            for t in range(UNITS):
+                lag = SCALAR_LAG if squared_by_scalar(t) else 2
+                if t + lag == i:
+                    square(t)
+                    fold(t)
+            for t in range(UNITS):
+                lag = SCALAR_LAG if squared_by_scalar(t) else 2
+                if t + lag + 2 == i:
+                    finish(t)
+        for t in range(UNITS):
+            sum_logs(t)
 
         shape = [P, ROW_TILES, CLUSTERS]
         z = keep.tile(shape, F32)
-        nc.vector.tensor_tensor(
+        nc.vector.scalar_tensor_tensor(
             out=z[:],
-            in0=logits_bc[:].unsqueeze(1).to_broadcast(shape),
-            in1=sums[:].rearrange("p k j -> p j k"),
-            op=ALU.subtract,
+            in0=sums[:].rearrange("p k j -> p j k"),
+            scalar=-0.5,
+            in1=log_sums[:].rearrange("p k j -> p j k"),
+            op0=ALU.mult,
+            op1=ALU.add,
         )
+        nc.vector.tensor_tensor(out=z[:], in0=z[:], in1=base[:].unsqueeze(1).to_broadcast(shape), op=ALU.add)
         top = keep.tile([P, ROW_TILES], F32)
         nc.vector.tensor_reduce(out=top[:], in_=z[:], axis=AX.X, op=ALU.max)
         nc.vector.tensor_tensor(

@@ -27,8 +27,11 @@ TILES_PER_HALF = HALF // P
 PAIRS_PER_HALF = HALF // (2 * P)
 UNITS = HALVES * CLUSTERS
 
-RING = 12
-SCALAR_LAG = 5
+RATIO_RING = 7
+TERM_RING = 5
+VECTOR_LAG = 5
+SQUARE_LAG = 7
+LOGS_A_STEP = 7
 
 EPS = 0.001
 TINY = 2.0**-60
@@ -46,7 +49,7 @@ def part(i, size):
 
 
 def squared_by_scalar(t):
-    return t % 2 == 1 and t < 30
+    return t < 24 and t % 4 != 3
 
 
 def tile_deepgmm_pa_kernel(
@@ -142,16 +145,6 @@ def tile_deepgmm_pa_kernel(
                     scales=sig_scales[:, g, :],
                     in_=sig_grouped[:, g].rearrange("p d t -> p (d t)"),
                 )
-            for g in range(PASSES):
-                nc.gpsimd.tensor_scalar(
-                    out=mu_grouped[:, g],
-                    in0=mu_raw[:, g].rearrange("p t d -> p d t"),
-                    scalar1=1.0,
-                    scalar2=0.0,
-                    op0=ALU.mult,
-                    op1=ALU.add,
-                )
-
             y_words = y_raw[:].bitcast(F32)
             y_pairs = y_grouped[:].bitcast(F32)
 
@@ -204,6 +197,14 @@ def tile_deepgmm_pa_kernel(
                 sig_accs[c, 1] = acc
                 matmul_y_moving(acc, sig_codes, sig_scales, c, 1)
 
+            for g in range(PASSES):
+                nc.vector.tensor_copy(out=mu_grouped[:, g], in_=mu_raw[:, g].rearrange("p t d -> p d t"))
+            for g in range(PASSES):
+                nc.vector.quantize_mx(
+                    out=mu_codes[:, g, :].bitcast(FP8X4),
+                    scales=mu_scales[:, g, :],
+                    in_=mu_grouped[:, g].rearrange("p d t -> p (d t)"),
+                )
             nc.vector.tensor_tensor(
                 out=mu_cols[:],
                 in0=cols[:, :, ROW_MU : ROW_MU + CLUSTERS],
@@ -211,12 +212,6 @@ def tile_deepgmm_pa_kernel(
                 op=ALU.subtract,
             )
             nc.vector.reciprocal(out=inv_phi[:], in_=cols[:, :, ROW_SIG : ROW_SIG + CLUSTERS])
-            for g in range(PASSES):
-                nc.vector.quantize_mx(
-                    out=mu_codes[:, g, :].bitcast(FP8X4),
-                    scales=mu_scales[:, g, :],
-                    in_=mu_grouped[:, g].rearrange("p d t -> p (d t)"),
-                )
             nc.vector.tensor_tensor(out=inv_phi_sq[:], in0=inv_phi[:], in1=inv_phi[:], op=ALU.mult)
 
             for h in range(HALVES):
@@ -232,14 +227,44 @@ def tile_deepgmm_pa_kernel(
                     nc.scalar.activation(
                         out=curve[:, c, part(h, HALF)], in_=curve[:, c, part(h, HALF)], func=ACT.Ln, bias=TINY
                     )
-                    nc.vector.scalar_tensor_tensor(
-                        out=neg_sig[:, c, part(h, HALF)],
-                        in0=sig_accs[c, h][:],
-                        scalar=cols[:, c, ROW_BE_SIG : ROW_BE_SIG + 1],
-                        in1=curve[:, c, part(h, HALF)],
-                        op0=ALU.subtract,
-                        op1=ALU.min,
+
+            def rows_of_mu(j):
+                pool = psum_b if j % 4 < 2 else psum_c
+                rows_mu = pool.tile([P, D], F32, tag="bank")
+                for g in range(PASSES):
+                    nc.tensor.matmul_mx(
+                        out=rows_mu[:],
+                        lhsT=y_codes[:, g, part(j, P)].bitcast(FP8X4),
+                        lhsT_scale=y_scales[:, g, part(j, P)],
+                        rhs=mu_codes[:, g, :].bitcast(FP8X4),
+                        rhs_scale=mu_scales[:, g, :],
+                        start=(g == 0),
+                        stop=(g == PASSES - 1),
                     )
+                rows_sb = stage.tile([P, D], F32)
+                nc.vector.tensor_tensor(out=rows_sb[:], in0=rows_mu[:], in1=be_mu_bc[:], op=ALU.add)
+                nc.sync.dma_start(out=out_0[part(j, P), :], in_=rows_sb[:])
+
+            def soft(acc, c, h):
+                nc.vector.scalar_tensor_tensor(
+                    out=neg_sig[:, c, part(h, HALF)],
+                    in0=acc[:],
+                    scalar=cols[:, c, ROW_BE_SIG : ROW_BE_SIG + 1],
+                    in1=curve[:, c, part(h, HALF)],
+                    op0=ALU.subtract,
+                    op1=ALU.min,
+                )
+
+            for j in range(2):
+                rows_of_mu(j)
+            for c in range(D_CHUNKS):
+                soft(sig_accs[c, 0], c, 0)
+            for c in range(D_CHUNKS):
+                acc = psum_c.tile([P, HALF], F32, tag="bank")
+                matmul_y_moving(acc, sig_codes, sig_scales, c, 1)
+                soft(acc, c, 1)
+            for j in range(2, ROW_TILES):
+                rows_of_mu(j)
             for h in range(HALVES):
                 nc.scalar.activation(
                     out=curve[:, :, part(h, HALF)],
@@ -250,22 +275,6 @@ def tile_deepgmm_pa_kernel(
                 )
             nc.scalar.activation(out=log_phi[:], in_=cols[:, :, ROW_SIG : ROW_SIG + CLUSTERS], func=ACT.Ln)
 
-        for j in range(ROW_TILES):
-            rows_mu = psum_a.tile([P, D], F32, tag="bank")
-            for g in range(PASSES):
-                nc.tensor.matmul_mx(
-                    out=rows_mu[:],
-                    lhsT=y_codes[:, g, part(j, P)].bitcast(FP8X4),
-                    lhsT_scale=y_scales[:, g, part(j, P)],
-                    rhs=mu_codes[:, g, :].bitcast(FP8X4),
-                    rhs_scale=mu_scales[:, g, :],
-                    start=(g == 0),
-                    stop=(g == PASSES - 1),
-                )
-            rows_sb = stage.tile([P, D], F32)
-            nc.vector.tensor_tensor(out=rows_sb[:], in0=rows_mu[:], in1=be_mu_bc[:], op=ALU.add)
-            nc.sync.dma_start(out=out_0[part(j, P), :], in_=rows_sb[:])
-
         mu_accs = {}
 
         def project_mu(h):
@@ -274,10 +283,9 @@ def tile_deepgmm_pa_kernel(
                 mu_accs[c, h] = acc
                 matmul_y_moving(acc, mu_codes, mu_scales, c, h)
 
-        project_mu(0)
-
         for j in range(ROW_TILES):
-            rows_t = psum_b.tile([P, D], F32, tag="bank")
+            pool = psum_b if j % 4 < 2 else psum_c
+            rows_t = pool.tile([P, D], F32, tag="bank")
             for c in range(D_CHUNKS):
                 nc.tensor.transpose(out=rows_t[:, part(c, P)], in_=neg_sig[:, c, part(j, P)], identity=ident_f32[:])
             rows_sb = stage.tile([P, D], F32)
@@ -285,6 +293,8 @@ def tile_deepgmm_pa_kernel(
                 out=rows_sb[:], in0=rows_t[:], scalar1=-1.0, scalar2=EPS, op0=ALU.mult, op1=ALU.add
             )
             nc.sync.dma_start(out=out_1[part(j, P), :], in_=rows_sb[:])
+
+        project_mu(0)
 
         phi_sums = psum_c.tile([P, CLUSTERS], F32, tag="bank")
         for c in range(D_CHUNKS):
@@ -294,15 +304,18 @@ def tile_deepgmm_pa_kernel(
         base = keep.tile([P, CLUSTERS], F32)
         nc.vector.tensor_tensor(out=base[:], in0=logits_bc[:], in1=phi_sums[:], op=ALU.subtract)
 
-        ring = ctx.enter_context(tc.tile_pool(name="ring", bufs=RING, reuse_waits="tile"))
-        pair_ring = ctx.enter_context(tc.tile_pool(name="pair_ring", bufs=2, reuse_waits="tile"))
+        ratio_ring = ctx.enter_context(tc.tile_pool(name="ratio_ring", bufs=RATIO_RING, reuse_waits="tile"))
+        term_ring = ctx.enter_context(tc.tile_pool(name="term_ring", bufs=TERM_RING, reuse_waits="tile"))
+        pair_pool = ctx.enter_context(tc.tile_pool(name="pair_pool", bufs=1, reuse_waits="tile"))
+        ratio_tiles = {}
+        pair_tiles = {}
         tiles = {}
         banks = {}
 
         def ratios(t):
             h, k = divmod(t, CLUSTERS)
-            tile = ring.tile([P, D_CHUNKS, HALF], F32)
-            tiles[t] = tile
+            tile = ratio_ring.tile([P, D_CHUNKS, HALF], F32)
+            ratio_tiles[t] = tile
             for c in range(D_CHUNKS):
                 nc.scalar.activation(
                     out=tile[:, c, :],
@@ -312,19 +325,27 @@ def tile_deepgmm_pa_kernel(
                     bias=log_phi[:, c, k : k + 1],
                 )
 
-        def multiply_ratios(t):
-            pairs = pair_ring.tile([P, 2, HALF], F32)
-            nc.gpsimd.tensor_tensor(out=pairs[:], in0=tiles[t][:, 0:2, :], in1=tiles[t][:, 2:4, :], op=ALU.mult)
-            nc.gpsimd.tensor_tensor(out=products[:, t, :], in0=pairs[:, 0, :], in1=pairs[:, 1, :], op=ALU.mult)
+        def multiply_pairs(t):
+            pairs = pair_pool.tile([P, 2, HALF], F32)
+            pair_tiles[t] = pairs
+            nc.gpsimd.tensor_tensor(
+                out=pairs[:], in0=ratio_tiles[t][:, 0:2, :], in1=ratio_tiles[t][:, 2:4, :], op=ALU.mult
+            )
+
+        def multiply_quads(t):
+            pairs = pair_tiles[t]
+            nc.vector.tensor_tensor(out=products[:, t, :], in0=pairs[:, 0, :], in1=pairs[:, 1, :], op=ALU.mult)
 
         def weigh(t):
             h, k = divmod(t, CLUSTERS)
+            tile = term_ring.tile([P, D_CHUNKS, HALF], F32)
+            tiles[t] = tile
             for c in range(D_CHUNKS):
                 nc.vector.scalar_tensor_tensor(
-                    out=tiles[t][:, c, :],
+                    out=tile[:, c, :],
                     in0=mu_accs[c, h][:],
                     scalar=mu_cols[:, c, k : k + 1],
-                    in1=tiles[t][:, c, :],
+                    in1=ratio_tiles[t][:, c, :],
                     op0=ALU.subtract,
                     op1=ALU.mult,
                 )
@@ -382,24 +403,31 @@ def tile_deepgmm_pa_kernel(
                     accum_out=log_sums[:, k, jj : jj + 1],
                 )
 
-        for i in range(UNITS + SCALAR_LAG + 2):
+        logged = 0
+        for i in range(UNITS + SQUARE_LAG + 3):
             if i < UNITS:
                 ratios(i)
-                multiply_ratios(i)
-            if 0 <= i - 1 < UNITS:
-                if i - 1 == CLUSTERS:
+            if i >= UNITS - 1:
+                for t in range(logged, min(logged + LOGS_A_STEP, UNITS)):
+                    if t < i - VECTOR_LAG:
+                        sum_logs(t)
+                        logged = t + 1
+            t = i - VECTOR_LAG
+            if 0 <= t < UNITS:
+                if t == CLUSTERS:
                     project_mu(1)
-                weigh(i - 1)
+                multiply_pairs(t)
+                weigh(t)
             for t in range(UNITS):
-                lag = SCALAR_LAG if squared_by_scalar(t) else 2
-                if t + lag == i:
+                if i == t + (SQUARE_LAG if squared_by_scalar(t) else VECTOR_LAG):
                     square(t)
                     fold(t)
+            if 0 <= i - VECTOR_LAG < UNITS:
+                multiply_quads(i - VECTOR_LAG)
             for t in range(UNITS):
-                lag = SCALAR_LAG if squared_by_scalar(t) else 2
-                if t + lag + 2 == i:
+                if i == t + (SQUARE_LAG if squared_by_scalar(t) else VECTOR_LAG) + 1:
                     finish(t)
-        for t in range(UNITS):
+        for t in range(logged, UNITS):
             sum_logs(t)
 
         shape = [P, ROW_TILES, CLUSTERS]

@@ -27,11 +27,11 @@ TILES_PER_HALF = HALF // P
 PAIRS_PER_HALF = HALF // (2 * P)
 UNITS = HALVES * CLUSTERS
 
-RATIO_RING = 7
-TERM_RING = 5
-VECTOR_LAG = 5
-SQUARE_LAG = 7
-LOGS_A_STEP = 7
+RATIO_RING = 8
+TERM_RING = 6
+VECTOR_LAG = 3
+SQUARE_LAG = 4
+LOGS_A_STEP = 13
 
 EPS = 0.001
 TINY = 2.0**-60
@@ -59,10 +59,9 @@ def tile_deepgmm_pa_kernel(
     with ExitStack() as ctx:
         ctx.enter_context(tc.manual_schedule())
         keep = ctx.enter_context(tc.tile_pool(name="keep", bufs=1))
-        stage = ctx.enter_context(tc.tile_pool(name="stage", bufs=8))
+        stage = ctx.enter_context(tc.tile_pool(name="stage", bufs=4))
         psum_a = ctx.enter_context(tc.psum_pool(name="psum_a", bufs=4))
-        psum_b = ctx.enter_context(tc.psum_pool(name="psum_b", bufs=2))
-        psum_c = ctx.enter_context(tc.psum_pool(name="psum_c", bufs=2))
+        psum_b = ctx.enter_context(tc.psum_pool(name="psum_b", bufs=4))
 
         ident_f32 = keep.tile([P, P], F32)
         make_identity(nc, ident_f32[:])
@@ -89,7 +88,6 @@ def tile_deepgmm_pa_kernel(
         logits_bc = keep.tile([P, CLUSTERS], BF16)
         be_mu_bc = keep.tile([P, D], BF16)
         curve = keep.tile([P, D_CHUNKS, ROWS], F32)
-        neg_sig = keep.tile([P, D_CHUNKS, ROWS], F32)
         products = keep.tile([P, UNITS, HALF], F32)
         sums = keep.tile([P, CLUSTERS, ROW_TILES], F32)
         y_codes = keep.tile([P, PASSES, ROWS], U32, align_bytes=64)
@@ -119,6 +117,7 @@ def tile_deepgmm_pa_kernel(
             sig_scales = load.tile([P, PASSES, D], U8, align_bytes=64)
             mu_raw = load.tile([P, PASSES, PACK, D], BF16)
             mu_grouped = load.tile([P, PASSES, D, PACK], BF16, align_bytes=64)
+            neg_sig = load.tile([P, D_CHUNKS, ROWS], F32)
 
             y_view = Y.rearrange("(j p) y -> p j y", p=P)
             sig_view = We_sig.rearrange("(g p t) d -> p g t d", g=PASSES, p=P, t=PACK)
@@ -177,7 +176,7 @@ def tile_deepgmm_pa_kernel(
             for pair in range(PAIRS_PER_HALF, ROW_TILES // 2):
                 turn_y(pair, psum_b)
 
-            params_t = psum_c.tile([P, D_CHUNKS, P], BF16, tag="bank")
+            params_t = psum_b.tile([P, D_CHUNKS, P], BF16, tag="bank")
             for c in range(D_CHUNKS):
                 nc.tensor.transpose(out=params_t[:, c, :], in_=param_rows[:, part(c, P)], identity=ident_bf16[:])
             nc.vector.tensor_copy(out=cols[:], in_=params_t[:])
@@ -192,8 +191,7 @@ def tile_deepgmm_pa_kernel(
                 matmul_y_moving(acc, sig_codes, sig_scales, c, 0)
             quantise_y(1)
             for c in range(D_CHUNKS):
-                pool = psum_b if c < 2 else psum_c
-                acc = pool.tile([P, HALF], F32, tag="bank")
+                acc = psum_b.tile([P, HALF], F32, tag="bank")
                 sig_accs[c, 1] = acc
                 matmul_y_moving(acc, sig_codes, sig_scales, c, 1)
 
@@ -229,8 +227,7 @@ def tile_deepgmm_pa_kernel(
                     )
 
             def rows_of_mu(j):
-                pool = psum_b if j % 4 < 2 else psum_c
-                rows_mu = pool.tile([P, D], F32, tag="bank")
+                rows_mu = psum_b.tile([P, D], F32, tag="bank")
                 for g in range(PASSES):
                     nc.tensor.matmul_mx(
                         out=rows_mu[:],
@@ -260,7 +257,7 @@ def tile_deepgmm_pa_kernel(
             for c in range(D_CHUNKS):
                 soft(sig_accs[c, 0], c, 0)
             for c in range(D_CHUNKS):
-                acc = psum_c.tile([P, HALF], F32, tag="bank")
+                acc = psum_b.tile([P, HALF], F32, tag="bank")
                 matmul_y_moving(acc, sig_codes, sig_scales, c, 1)
                 soft(acc, c, 1)
             for j in range(2, ROW_TILES):
@@ -275,6 +272,16 @@ def tile_deepgmm_pa_kernel(
                 )
             nc.scalar.activation(out=log_phi[:], in_=cols[:, :, ROW_SIG : ROW_SIG + CLUSTERS], func=ACT.Ln)
 
+            for j in range(ROW_TILES):
+                rows_t = psum_b.tile([P, D], F32, tag="bank")
+                for c in range(D_CHUNKS):
+                    nc.tensor.transpose(out=rows_t[:, part(c, P)], in_=neg_sig[:, c, part(j, P)], identity=ident_f32[:])
+                rows_sb = stage.tile([P, D], F32)
+                nc.vector.tensor_scalar(
+                    out=rows_sb[:], in0=rows_t[:], scalar1=-1.0, scalar2=EPS, op0=ALU.mult, op1=ALU.add
+                )
+                nc.sync.dma_start(out=out_1[part(j, P), :], in_=rows_sb[:])
+
         mu_accs = {}
 
         def project_mu(h):
@@ -283,20 +290,9 @@ def tile_deepgmm_pa_kernel(
                 mu_accs[c, h] = acc
                 matmul_y_moving(acc, mu_codes, mu_scales, c, h)
 
-        for j in range(ROW_TILES):
-            pool = psum_b if j % 4 < 2 else psum_c
-            rows_t = pool.tile([P, D], F32, tag="bank")
-            for c in range(D_CHUNKS):
-                nc.tensor.transpose(out=rows_t[:, part(c, P)], in_=neg_sig[:, c, part(j, P)], identity=ident_f32[:])
-            rows_sb = stage.tile([P, D], F32)
-            nc.vector.tensor_scalar(
-                out=rows_sb[:], in0=rows_t[:], scalar1=-1.0, scalar2=EPS, op0=ALU.mult, op1=ALU.add
-            )
-            nc.sync.dma_start(out=out_1[part(j, P), :], in_=rows_sb[:])
-
         project_mu(0)
 
-        phi_sums = psum_c.tile([P, CLUSTERS], F32, tag="bank")
+        phi_sums = psum_b.tile([P, CLUSTERS], F32, tag="bank")
         for c in range(D_CHUNKS):
             nc.tensor.matmul(
                 out=phi_sums[:], lhsT=ones[:], rhs=log_phi[:, c, :], start=(c == 0), stop=(c == D_CHUNKS - 1)
@@ -325,16 +321,18 @@ def tile_deepgmm_pa_kernel(
                     bias=log_phi[:, c, k : k + 1],
                 )
 
-        def multiply_pairs(t):
-            pairs = pair_pool.tile([P, 2, HALF], F32)
-            pair_tiles[t] = pairs
-            nc.gpsimd.tensor_tensor(
-                out=pairs[:], in0=ratio_tiles[t][:, 0:2, :], in1=ratio_tiles[t][:, 2:4, :], op=ALU.mult
-            )
+        def multiply_pairs(p):
+            pairs = pair_pool.tile([P, 2, 2, HALF], F32)
+            pair_tiles[p] = pairs
+            for i in range(2):
+                ratio = ratio_tiles[2 * p + i]
+                nc.gpsimd.tensor_tensor(out=pairs[:, i], in0=ratio[:, 0:2, :], in1=ratio[:, 2:4, :], op=ALU.mult)
 
-        def multiply_quads(t):
-            pairs = pair_tiles[t]
-            nc.vector.tensor_tensor(out=products[:, t, :], in0=pairs[:, 0, :], in1=pairs[:, 1, :], op=ALU.mult)
+        def multiply_quads(p):
+            pairs = pair_tiles[p]
+            nc.vector.tensor_tensor(
+                out=products[:, part(p, 2), :], in0=pairs[:, :, 0, :], in1=pairs[:, :, 1, :], op=ALU.mult
+            )
 
         def weigh(t):
             h, k = divmod(t, CLUSTERS)
@@ -391,7 +389,7 @@ def tile_deepgmm_pa_kernel(
 
         def sum_logs(t):
             h, k = divmod(t, CLUSTERS)
-            turned = psum_c.tile([P, TILES_PER_HALF, P], F32, tag="bank")
+            turned = psum_b.tile([P, TILES_PER_HALF, P], F32, tag="bank")
             for j in range(TILES_PER_HALF):
                 nc.tensor.transpose(out=turned[:, j, :], in_=products[:, t, part(j, P)], identity=ident_f32[:])
             for j in range(TILES_PER_HALF):
@@ -404,29 +402,33 @@ def tile_deepgmm_pa_kernel(
                 )
 
         logged = 0
-        for i in range(UNITS + SQUARE_LAG + 3):
-            if i < UNITS:
-                ratios(i)
-            if i >= UNITS - 1:
+        steps = UNITS // 2
+        for i in range(steps + SQUARE_LAG + 2):
+            if i < steps:
+                ratios(2 * i)
+                ratios(2 * i + 1)
+            if i >= steps - 1:
                 for t in range(logged, min(logged + LOGS_A_STEP, UNITS)):
-                    if t < i - VECTOR_LAG:
+                    if t // 2 < i - VECTOR_LAG:
                         sum_logs(t)
                         logged = t + 1
-            t = i - VECTOR_LAG
-            if 0 <= t < UNITS:
-                if t == CLUSTERS:
+            p = i - VECTOR_LAG
+            if 0 <= p < steps:
+                multiply_pairs(p)
+                weigh(2 * p)
+                weigh(2 * p + 1)
+                if 2 * p + 2 == CLUSTERS:
                     project_mu(1)
-                multiply_pairs(t)
-                weigh(t)
+            due = lambda t, lag: i == t // 2 + (SQUARE_LAG if squared_by_scalar(t) else VECTOR_LAG) + lag
             for t in range(UNITS):
-                if i == t + (SQUARE_LAG if squared_by_scalar(t) else VECTOR_LAG):
+                if due(t, 1):
+                    finish(t)
+            for t in range(UNITS):
+                if due(t, 0):
                     square(t)
                     fold(t)
-            if 0 <= i - VECTOR_LAG < UNITS:
-                multiply_quads(i - VECTOR_LAG)
-            for t in range(UNITS):
-                if i == t + (SQUARE_LAG if squared_by_scalar(t) else VECTOR_LAG) + 1:
-                    finish(t)
+            if 0 <= p < steps:
+                multiply_quads(p)
         for t in range(logged, UNITS):
             sum_logs(t)
 

@@ -31,7 +31,7 @@ RATIO_RING = 8
 TERM_RING = 6
 VECTOR_LAG = 3
 SQUARE_LAG = 4
-LOGS_A_STEP = 13
+LOGS_A_STEP = 7
 
 EPS = 0.001
 TINY = 2.0**-60
@@ -49,7 +49,7 @@ def part(i, size):
 
 
 def squared_by_scalar(t):
-    return t < 24 and t % 4 != 3
+    return t % 2 == 1 or t % 8 == 2
 
 
 def tile_deepgmm_pa_kernel(
@@ -226,6 +226,14 @@ def tile_deepgmm_pa_kernel(
                         out=curve[:, c, part(h, HALF)], in_=curve[:, c, part(h, HALF)], func=ACT.Ln, bias=TINY
                     )
 
+            mu_accs = {}
+
+            def project_mu(h):
+                for c in range(D_CHUNKS):
+                    acc = psum_a.tile([P, HALF], F32, tag="bank")
+                    mu_accs[c, h] = acc
+                    matmul_y_moving(acc, mu_codes, mu_scales, c, h)
+
             def rows_of_mu(j):
                 rows_mu = psum_b.tile([P, D], F32, tag="bank")
                 for g in range(PASSES):
@@ -260,6 +268,7 @@ def tile_deepgmm_pa_kernel(
                 acc = psum_b.tile([P, HALF], F32, tag="bank")
                 matmul_y_moving(acc, sig_codes, sig_scales, c, 1)
                 soft(acc, c, 1)
+            project_mu(0)
             for j in range(2, ROW_TILES):
                 rows_of_mu(j)
             for h in range(HALVES):
@@ -281,16 +290,6 @@ def tile_deepgmm_pa_kernel(
                     out=rows_sb[:], in0=rows_t[:], scalar1=-1.0, scalar2=EPS, op0=ALU.mult, op1=ALU.add
                 )
                 nc.sync.dma_start(out=out_1[part(j, P), :], in_=rows_sb[:])
-
-        mu_accs = {}
-
-        def project_mu(h):
-            for c in range(D_CHUNKS):
-                acc = psum_a.tile([P, HALF], F32, tag="bank")
-                mu_accs[c, h] = acc
-                matmul_y_moving(acc, mu_codes, mu_scales, c, h)
-
-        project_mu(0)
 
         phi_sums = psum_b.tile([P, CLUSTERS], F32, tag="bank")
         for c in range(D_CHUNKS):
@@ -407,11 +406,6 @@ def tile_deepgmm_pa_kernel(
             if i < steps:
                 ratios(2 * i)
                 ratios(2 * i + 1)
-            if i >= steps - 1:
-                for t in range(logged, min(logged + LOGS_A_STEP, UNITS)):
-                    if t // 2 < i - VECTOR_LAG:
-                        sum_logs(t)
-                        logged = t + 1
             p = i - VECTOR_LAG
             if 0 <= p < steps:
                 multiply_pairs(p)
@@ -426,6 +420,13 @@ def tile_deepgmm_pa_kernel(
             for t in range(UNITS):
                 if due(t, 0):
                     square(t)
+            if i >= steps - 1:
+                for t in range(logged, min(logged + LOGS_A_STEP, UNITS)):
+                    if t // 2 < i - VECTOR_LAG:
+                        sum_logs(t)
+                        logged = t + 1
+            for t in range(UNITS):
+                if due(t, 0):
                     fold(t)
             if 0 <= p < steps:
                 multiply_quads(p)

@@ -49,7 +49,7 @@ def part(i, size):
 
 
 def squared_by_scalar(t):
-    return t % 2 == 1 or t % 8 == 2
+    return t % 2 == 1 or t % 6 == 2
 
 
 def tile_deepgmm_pa_kernel(
@@ -196,7 +196,14 @@ def tile_deepgmm_pa_kernel(
                 matmul_y_moving(acc, sig_codes, sig_scales, c, 1)
 
             for g in range(PASSES):
-                nc.vector.tensor_copy(out=mu_grouped[:, g], in_=mu_raw[:, g].rearrange("p t d -> p d t"))
+                nc.gpsimd.tensor_scalar(
+                    out=mu_grouped[:, g],
+                    in0=mu_raw[:, g].rearrange("p t d -> p d t"),
+                    scalar1=1.0,
+                    scalar2=0.0,
+                    op0=ALU.mult,
+                    op1=ALU.add,
+                )
             for g in range(PASSES):
                 nc.vector.quantize_mx(
                     out=mu_codes[:, g, :].bitcast(FP8X4),
@@ -433,6 +440,8 @@ def tile_deepgmm_pa_kernel(
         for t in range(logged, UNITS):
             sum_logs(t)
 
+        nc.scalar.activation(out=warm[:], in_=ones[:, 0:1], func=ACT.Exp)
+
         shape = [P, ROW_TILES, CLUSTERS]
         z = keep.tile(shape, F32)
         nc.vector.scalar_tensor_tensor(
@@ -451,6 +460,7 @@ def tile_deepgmm_pa_kernel(
         )
         weights = keep.tile(shape, F32)
         nc.scalar.activation(out=weights[:], in_=z[:], func=ACT.Exp)
+        nc.scalar.activation(out=warm[:], in_=ones[:, 0:1], func=ACT.Ln)
         norm = keep.tile([P, ROW_TILES], F32)
         nc.vector.tensor_reduce(out=norm[:], in_=weights[:], axis=AX.X, op=ALU.add)
         nc.scalar.activation(out=norm[:], in_=norm[:], func=ACT.Ln)

@@ -196,14 +196,7 @@ def tile_deepgmm_pa_kernel(
                 matmul_y_moving(acc, sig_codes, sig_scales, c, 1)
 
             for g in range(PASSES):
-                nc.gpsimd.tensor_scalar(
-                    out=mu_grouped[:, g],
-                    in0=mu_raw[:, g].rearrange("p t d -> p d t"),
-                    scalar1=1.0,
-                    scalar2=0.0,
-                    op0=ALU.mult,
-                    op1=ALU.add,
-                )
+                nc.vector.tensor_copy(out=mu_grouped[:, g], in_=mu_raw[:, g].rearrange("p t d -> p d t"))
             for g in range(PASSES):
                 nc.vector.quantize_mx(
                     out=mu_codes[:, g, :].bitcast(FP8X4),

from contextlib import ExitStack

import concourse.mybir as mybir
from concourse.masks import make_identity

F32 = mybir.dt.float32
BF16 = mybir.dt.bfloat16
U32 = mybir.dt.uint32
U8 = mybir.dt.uint8
FP8X4 = mybir.dt.float8_e4m3fn_x4
ACT = mybir.ActivationFunctionType
ALU = mybir.AluOpType
AX = mybir.AxisListType

P = 128
ROWS = 1024
KDIM = 1024
D = 512
CLUSTERS = 16
ROW_TILES = ROWS // P
D_CHUNKS = D // P
PACK = 4
PASSES = KDIM // (P * PACK)
HALF = 512
HALVES = ROWS // HALF
TILES_PER_HALF = HALF // P
PAIRS_PER_HALF = HALF // (2 * P)
UNITS = HALVES * CLUSTERS

RATIO_RING = 8
TERM_RING = 6
VECTOR_LAG = 3
SQUARE_LAG = 4
LOGS_A_STEP = 7

EPS = 0.001
TINY = 2.0**-60

ROW_MU = 0
ROW_SIG = CLUSTERS
ROW_BE_MU = 2 * CLUSTERS
ROW_BE_SIG = 2 * CLUSTERS + 1

FLOPS = 2 * 2 * ROWS * KDIM * D


def part(i, size):
    return slice(i * size, (i + 1) * size)


def squared_by_scalar(t):
    return t % 2 == 1 or t % 6 == 2


def tile_deepgmm_pa_kernel(
    tc, Y, We_mu, be_mu, We_sig, be_sig, phi_mus, phi_sigs, phi_logits, out_0, out_1, out_2
):
    nc = tc.nc
    with ExitStack() as ctx:
        ctx.enter_context(tc.manual_schedule())
        keep = ctx.enter_context(tc.tile_pool(name="keep", bufs=1))
        stage = ctx.enter_context(tc.tile_pool(name="stage", bufs=4))
        psum_a = ctx.enter_context(tc.psum_pool(name="psum_a", bufs=4))
        psum_b = ctx.enter_context(tc.psum_pool(name="psum_b", bufs=4))

        ident_f32 = keep.tile([P, P], F32)
        make_identity(nc, ident_f32[:])
        ident_bf16 = keep.tile([P, P], BF16)
        make_identity(nc, ident_bf16[:])
        ones = keep.tile([P, P], F32)
        nc.vector.memset(ones[:], 1.0)
        warm = keep.tile([P, 1], F32)
        nc.scalar.activation(out=warm[:], in_=ones[:, 0:1], func=ACT.Sigmoid)

        param_rows = keep.tile([P, D], BF16)
        nc.vector.memset(param_rows[:], 0.0)
        nc.scalar.dma_start(out=param_rows[ROW_MU : ROW_MU + CLUSTERS, :], in_=phi_mus)
        nc.scalar.dma_start(out=param_rows[ROW_SIG : ROW_SIG + CLUSTERS, :], in_=phi_sigs)
        nc.scalar.dma_start(out=param_rows[ROW_BE_MU : ROW_BE_MU + 1, :], in_=be_mu.unsqueeze(0))
        nc.scalar.dma_start(out=param_rows[ROW_BE_SIG : ROW_BE_SIG + 1, :], in_=be_sig.unsqueeze(0))

        cols = keep.tile([P, D_CHUNKS, P], F32)
        neg_be_sig = keep.tile([P, D_CHUNKS], F32)
        mu_cols = keep.tile([P, D_CHUNKS, CLUSTERS], F32)
        inv_phi = keep.tile([P, D_CHUNKS, CLUSTERS], F32)
        inv_phi_sq = keep.tile([P, D_CHUNKS, CLUSTERS], F32)
        log_phi = keep.tile([P, D_CHUNKS, CLUSTERS], F32)
        logits_bc = keep.tile([P, CLUSTERS], BF16)
        be_mu_bc = keep.tile([P, D], BF16)
        curve = keep.tile([P, D_CHUNKS, ROWS], F32)
        products = keep.tile([P, UNITS, HALF], F32)
        sums = keep.tile([P, CLUSTERS, ROW_TILES], F32)
        y_codes = keep.tile([P, PASSES, ROWS], U32, align_bytes=64)
        y_scales = keep.tile([P, PASSES, ROWS], U8, align_bytes=64)
        mu_codes = keep.tile([P, PASSES, D], U32, align_bytes=64)
        mu_scales = keep.tile([P, PASSES, D], U8, align_bytes=64)

        def matmul_y_moving(acc, codes, scales, c, h):
            for g in range(PASSES):
                nc.tensor.matmul_mx(
                    out=acc[:],
                    lhsT=codes[:, g, part(c, P)].bitcast(FP8X4),
                    lhsT_scale=scales[:, g, part(c, P)],
                    rhs=y_codes[:, g, part(h, HALF)].bitcast(FP8X4),
                    rhs_scale=y_scales[:, g, part(h, HALF)],
                    start=(g == 0),
                    stop=(g == PASSES - 1),
                )

        with ExitStack() as head:
            load = head.enter_context(tc.tile_pool(name="load", bufs=1))
            y_raw = load.tile([P, ROW_TILES, KDIM], BF16)
            y_grouped = load.tile([P, PASSES, ROWS, PACK], BF16, align_bytes=64)
            sig_raw = load.tile([P, PASSES, PACK, D], BF16)
            sig_grouped = load.tile([P, PASSES, D, PACK], BF16, align_bytes=64)
            sig_codes = load.tile([P, PASSES, D], U32, align_bytes=64)
            sig_scales = load.tile([P, PASSES, D], U8, align_bytes=64)
            mu_raw = load.tile([P, PASSES, PACK, D], BF16)
            mu_grouped = load.tile([P, PASSES, D, PACK], BF16, align_bytes=64)
            neg_sig = load.tile([P, D_CHUNKS, ROWS], F32)

            y_view = Y.rearrange("(j p) y -> p j y", p=P)
            sig_view = We_sig.rearrange("(g p t) d -> p g t d", g=PASSES, p=P, t=PACK)
            for g in range(PASSES):
                nc.sync.dma_start(out=sig_raw[:, g], in_=sig_view[:, g])
                nc.sync.dma_start(out=y_raw[:, part(g, 2), :], in_=y_view[:, part(g, 2), :])
            for pair in range(PAIRS_PER_HALF, ROW_TILES // 2):
                nc.sync.dma_start(out=y_raw[:, part(pair, 2), :], in_=y_view[:, part(pair, 2), :])
            nc.sync.dma_start(out=mu_raw[:], in_=We_mu.rearrange("(g p t) d -> p g t d", g=PASSES, p=P, t=PACK))
            nc.sync.dma_start(out=be_mu_bc[:], in_=be_mu.partition_broadcast(P))
            nc.sync.dma_start(out=logits_bc[:], in_=phi_logits.partition_broadcast(P))

            for g in range(PASSES):
                nc.vector.tensor_scalar(
                    out=sig_grouped[:, g],
                    in0=sig_raw[:, g].rearrange("p t d -> p d t"),
                    scalar1=-1.0,
                    scalar2=None,
                    op0=ALU.mult,
                )
            for g in range(PASSES):
                nc.vector.quantize_mx(
                    out=sig_codes[:, g, :].bitcast(FP8X4),
                    scales=sig_scales[:, g, :],
                    in_=sig_grouped[:, g].rearrange("p d t -> p (d t)"),
                )
            y_words = y_raw[:].bitcast(F32)
            y_pairs = y_grouped[:].bitcast(F32)

            def turn_y(pair, pool):
                for g in range(PASSES):
                    y_t = pool.tile([P, 2, 2 * P], F32, tag="bank")
                    for u in range(2):
                        for jj in range(2):
                            nc.tensor.transpose(
                                out=y_t[:, u, part(jj, P)],
                                in_=y_words[:, 2 * pair + jj, 2 * P * g + u : 2 * P * (g + 1) : 2],
                                identity=ident_f32[:],
                            )
                    nc.scalar.copy(
                        out=y_pairs[:, g, part(pair, 2 * P), :],
                        in_=y_t[:].rearrange("p u n -> p n u"),
                    )

            def quantise_y(h):
                for g in range(PASSES):
                    nc.vector.quantize_mx(
                        out=y_codes[:, g, part(h, HALF)].bitcast(FP8X4),
                        scales=y_scales[:, g, part(h, HALF)],
                        in_=y_grouped[:, g, part(h, HALF), :].rearrange("p n t -> p (n t)"),
                    )

            for pair in range(PAIRS_PER_HALF):
                turn_y(pair, psum_a)
            quantise_y(0)
            for pair in range(PAIRS_PER_HALF, ROW_TILES // 2):
                turn_y(pair, psum_b)

            params_t = psum_b.tile([P, D_CHUNKS, P], BF16, tag="bank")
            for c in range(D_CHUNKS):
                nc.tensor.transpose(out=params_t[:, c, :], in_=param_rows[:, part(c, P)], identity=ident_bf16[:])
            nc.vector.tensor_copy(out=cols[:], in_=params_t[:])
            nc.vector.tensor_scalar(
                out=neg_be_sig[:], in0=cols[:, :, ROW_BE_SIG], scalar1=-1.0, scalar2=None, op0=ALU.mult
            )

            sig_accs = {}
            for c in range(D_CHUNKS):
                acc = psum_a.tile([P, HALF], F32, tag="bank")
                sig_accs[c, 0] = acc
                matmul_y_moving(acc, sig_codes, sig_scales, c, 0)
            quantise_y(1)
            for c in range(D_CHUNKS):
                acc = psum_b.tile([P, HALF], F32, tag="bank")
                sig_accs[c, 1] = acc
                matmul_y_moving(acc, sig_codes, sig_scales, c, 1)

            for g in range(PASSES):
                nc.vector.tensor_copy(out=mu_grouped[:, g], in_=mu_raw[:, g].rearrange("p t d -> p d t"))
            for g in range(PASSES):
                nc.vector.quantize_mx(
                    out=mu_codes[:, g, :].bitcast(FP8X4),
                    scales=mu_scales[:, g, :],
                    in_=mu_grouped[:, g].rearrange("p d t -> p (d t)"),
                )
            nc.vector.tensor_tensor(
                out=mu_cols[:],
                in0=cols[:, :, ROW_MU : ROW_MU + CLUSTERS],
                in1=cols[:, :, ROW_BE_MU : ROW_BE_MU + 1].to_broadcast([P, D_CHUNKS, CLUSTERS]),
                op=ALU.subtract,
            )
            nc.vector.reciprocal(out=inv_phi[:], in_=cols[:, :, ROW_SIG : ROW_SIG + CLUSTERS])
            nc.vector.tensor_tensor(out=inv_phi_sq[:], in0=inv_phi[:], in1=inv_phi[:], op=ALU.mult)

            for h in range(HALVES):
                for c in range(D_CHUNKS):
                    nc.scalar.activation(
                        out=curve[:, c, part(h, HALF)],
                        in_=sig_accs[c, h][:],
                        func=ACT.Sigmoid,
                        bias=neg_be_sig[:, c : c + 1],
                    )
            for h in range(HALVES):
                for c in range(D_CHUNKS):
                    nc.scalar.activation(
                        out=curve[:, c, part(h, HALF)], in_=curve[:, c, part(h, HALF)], func=ACT.Ln, bias=TINY
                    )

            mu_accs = {}

            def project_mu(h):
                for c in range(D_CHUNKS):
                    acc = psum_a.tile([P, HALF], F32, tag="bank")
                    mu_accs[c, h] = acc
                    matmul_y_moving(acc, mu_codes, mu_scales, c, h)

            def rows_of_mu(j):
                rows_mu = psum_b.tile([P, D], F32, tag="bank")
                for g in range(PASSES):
                    nc.tensor.matmul_mx(
                        out=rows_mu[:],
                        lhsT=y_codes[:, g, part(j, P)].bitcast(FP8X4),
                        lhsT_scale=y_scales[:, g, part(j, P)],
                        rhs=mu_codes[:, g, :].bitcast(FP8X4),
                        rhs_scale=mu_scales[:, g, :],
                        start=(g == 0),
                        stop=(g == PASSES - 1),
                    )
                rows_sb = stage.tile([P, D], F32)
                nc.vector.tensor_tensor(out=rows_sb[:], in0=rows_mu[:], in1=be_mu_bc[:], op=ALU.add)
                nc.sync.dma_start(out=out_0[part(j, P), :], in_=rows_sb[:])

            def soft(acc, c, h):
                nc.vector.scalar_tensor_tensor(
                    out=neg_sig[:, c, part(h, HALF)],
                    in0=acc[:],
                    scalar=cols[:, c, ROW_BE_SIG : ROW_BE_SIG + 1],
                    in1=curve[:, c, part(h, HALF)],
                    op0=ALU.subtract,
                    op1=ALU.min,
                )

            for j in range(2):
                rows_of_mu(j)
            for c in range(D_CHUNKS):
                soft(sig_accs[c, 0], c, 0)
            for c in range(D_CHUNKS):
                acc = psum_b.tile([P, HALF], F32, tag="bank")
                matmul_y_moving(acc, sig_codes, sig_scales, c, 1)
                soft(acc, c, 1)
            project_mu(0)
            for j in range(2, ROW_TILES):
                rows_of_mu(j)
            for h in range(HALVES):
                nc.scalar.activation(
                    out=curve[:, :, part(h, HALF)],
                    in_=neg_sig[:, :, part(h, HALF)],
                    func=ACT.Ln,
                    scale=-1.0,
                    bias=EPS,
                )
            nc.scalar.activation(out=log_phi[:], in_=cols[:, :, ROW_SIG : ROW_SIG + CLUSTERS], func=ACT.Ln)

            for j in range(ROW_TILES):
                rows_t = psum_b.tile([P, D], F32, tag="bank")
                for c in range(D_CHUNKS):
                    nc.tensor.transpose(out=rows_t[:, part(c, P)], in_=neg_sig[:, c, part(j, P)], identity=ident_f32[:])
                rows_sb = stage.tile([P, D], F32)
                nc.vector.tensor_scalar(
                    out=rows_sb[:], in0=rows_t[:], scalar1=-1.0, scalar2=EPS, op0=ALU.mult, op1=ALU.add
                )
                nc.sync.dma_start(out=out_1[part(j, P), :], in_=rows_sb[:])

        phi_sums = psum_b.tile([P, CLUSTERS], F32, tag="bank")
        for c in range(D_CHUNKS):
            nc.tensor.matmul(
                out=phi_sums[:], lhsT=ones[:], rhs=log_phi[:, c, :], start=(c == 0), stop=(c == D_CHUNKS - 1)
            )
        base = keep.tile([P, CLUSTERS], F32)
        nc.vector.tensor_tensor(out=base[:], in0=logits_bc[:], in1=phi_sums[:], op=ALU.subtract)

        ratio_ring = ctx.enter_context(tc.tile_pool(name="ratio_ring", bufs=RATIO_RING, reuse_waits="tile"))
        term_ring = ctx.enter_context(tc.tile_pool(name="term_ring", bufs=TERM_RING, reuse_waits="tile"))
        pair_pool = ctx.enter_context(tc.tile_pool(name="pair_pool", bufs=1, reuse_waits="tile"))
        ratio_tiles = {}
        pair_tiles = {}
        tiles = {}
        banks = {}

        def ratios(t):
            h, k = divmod(t, CLUSTERS)
            tile = ratio_ring.tile([P, D_CHUNKS, HALF], F32)
            ratio_tiles[t] = tile
            for c in range(D_CHUNKS):
                nc.scalar.activation(
                    out=tile[:, c, :],
                    in_=curve[:, c, part(h, HALF)],
                    func=ACT.Sigmoid,
                    scale=-1.0,
                    bias=log_phi[:, c, k : k + 1],
                )

        def multiply_pairs(p):
            pairs = pair_pool.tile([P, 2, 2, HALF], F32)
            pair_tiles[p] = pairs
            for i in range(2):
                ratio = ratio_tiles[2 * p + i]
                nc.gpsimd.tensor_tensor(out=pairs[:, i], in0=ratio[:, 0:2, :], in1=ratio[:, 2:4, :], op=ALU.mult)

        def multiply_quads(p):
            pairs = pair_tiles[p]
            nc.vector.tensor_tensor(
                out=products[:, part(p, 2), :], in0=pairs[:, :, 0, :], in1=pairs[:, :, 1, :], op=ALU.mult
            )

        def weigh(t):
            h, k = divmod(t, CLUSTERS)
            tile = term_ring.tile([P, D_CHUNKS, HALF], F32)
            tiles[t] = tile
            for c in range(D_CHUNKS):
                nc.vector.scalar_tensor_tensor(
                    out=tile[:, c, :],
                    in0=mu_accs[c, h][:],
                    scalar=mu_cols[:, c, k : k + 1],
                    in1=ratio_tiles[t][:, c, :],
                    op0=ALU.subtract,
                    op1=ALU.mult,
                )

        def square(t):
            k = t % CLUSTERS
            for c in range(D_CHUNKS):
                if squared_by_scalar(t):
                    nc.scalar.activation(
                        out=tiles[t][:, c, :], in_=tiles[t][:, c, :], func=ACT.Square, scale=inv_phi[:, c, k : k + 1]
                    )
                else:
                    nc.vector.scalar_tensor_tensor(
                        out=tiles[t][:, c, :],
                        in0=tiles[t][:, c, :],
                        scalar=inv_phi_sq[:, c, k : k + 1],
                        in1=tiles[t][:, c, :],
                        op0=ALU.mult,
                        op1=ALU.mult,
                    )

        def fold(t):
            bank = psum_b.tile([P, TILES_PER_HALF, P], F32, tag="bank")
            banks[t] = bank
            for c in range(D_CHUNKS):
                for j in range(TILES_PER_HALF):
                    nc.tensor.matmul(
                        out=bank[:, j, :],
                        lhsT=tiles[t][:, c, part(j, P)],
                        rhs=ident_f32[:],
                        is_transpose=True,
                        start=(c == 0 and j == 0),
                        stop=(c == D_CHUNKS - 1 and j == TILES_PER_HALF - 1),
                    )

        def finish(t):
            h, k = divmod(t, CLUSTERS)
            nc.vector.tensor_reduce(
                out=sums[:, k, part(h, TILES_PER_HALF)], in_=banks[t][:], axis=AX.X, op=ALU.add
            )

        log_sums = keep.tile([P, CLUSTERS, ROW_TILES], F32)

        def sum_logs(t):
            h, k = divmod(t, CLUSTERS)
            turned = psum_b.tile([P, TILES_PER_HALF, P], F32, tag="bank")
            for j in range(TILES_PER_HALF):
                nc.tensor.transpose(out=turned[:, j, :], in_=products[:, t, part(j, P)], identity=ident_f32[:])
            for j in range(TILES_PER_HALF):
                jj = h * TILES_PER_HALF + j
                nc.scalar.activation(
                    out=products[:, t, part(j, P)],
                    in_=turned[:, j, :],
                    func=ACT.Ln,
                    accum_out=log_sums[:, k, jj : jj + 1],
                )

        logged = 0
        steps = UNITS // 2
        for i in range(steps + SQUARE_LAG + 2):
            if i < steps:
                ratios(2 * i)
                ratios(2 * i + 1)
            p = i - VECTOR_LAG
            if 0 <= p < steps:
                multiply_pairs(p)
                weigh(2 * p)
                weigh(2 * p + 1)
                if 2 * p + 2 == CLUSTERS:
                    project_mu(1)
            due = lambda t, lag: i == t // 2 + (SQUARE_LAG if squared_by_scalar(t) else VECTOR_LAG) + lag
            for t in range(UNITS):
                if due(t, 1):
                    finish(t)
            for t in range(UNITS):
                if due(t, 0):
                    square(t)
            if i >= steps - 1:
                for t in range(logged, min(logged + LOGS_A_STEP, UNITS)):
                    if t // 2 < i - VECTOR_LAG:
                        sum_logs(t)
                        logged = t + 1
            for t in range(UNITS):
                if due(t, 0):
                    fold(t)
            if 0 <= p < steps:
                multiply_quads(p)
        for t in range(logged, UNITS):
            sum_logs(t)

        nc.scalar.activation(out=warm[:], in_=ones[:, 0:1], func=ACT.Exp)

        shape = [P, ROW_TILES, CLUSTERS]
        z = keep.tile(shape, F32)
        nc.vector.scalar_tensor_tensor(
            out=z[:],
            in0=sums[:].rearrange("p k j -> p j k"),
            scalar=-0.5,
            in1=log_sums[:].rearrange("p k j -> p j k"),
            op0=ALU.mult,
            op1=ALU.add,
        )
        nc.vector.tensor_tensor(out=z[:], in0=z[:], in1=base[:].unsqueeze(1).to_broadcast(shape), op=ALU.add)
        top = keep.tile([P, ROW_TILES], F32)
        nc.vector.tensor_reduce(out=top[:], in_=z[:], axis=AX.X, op=ALU.max)
        nc.vector.tensor_tensor(
            out=z[:], in0=z[:], in1=top[:].unsqueeze(2).to_broadcast(shape), op=ALU.subtract
        )
        weights = keep.tile(shape, F32)
        nc.scalar.activation(out=weights[:], in_=z[:], func=ACT.Exp)
        nc.scalar.activation(out=warm[:], in_=ones[:, 0:1], func=ACT.Ln)
        norm = keep.tile([P, ROW_TILES], F32)
        nc.vector.tensor_reduce(out=norm[:], in_=weights[:], axis=AX.X, op=ALU.add)
        nc.scalar.activation(out=norm[:], in_=norm[:], func=ACT.Ln)
        nc.vector.tensor_tensor(
            out=z[:], in0=z[:], in1=norm[:].unsqueeze(2).to_broadcast(shape), op=ALU.subtract
        )
        nc.sync.dma_start(out=out_2.rearrange("(j p) k -> p j k", p=P), in_=z[:])
